import numpy as np
import ml_dtypes


def mxq(x, axis, fmt="e4m3"):
    dtype, down = {"e4m3": (ml_dtypes.float8_e4m3fn, 7), "e5m2": (ml_dtypes.float8_e5m2, 14)}[fmt]
    v = np.moveaxis(np.asarray(x, np.float32).astype(ml_dtypes.bfloat16).astype(np.float64), axis, -1)
    blocks = v.reshape(v.shape[:-1] + (-1, 32))
    amax = np.abs(blocks).max(-1, keepdims=True)
    byte = np.maximum(np.where(amax > 0, np.frexp(amax)[1] - 1 + 127, 0) - down, 1)
    scale = np.exp2(byte - 127.0)
    codes = (blocks / scale).astype(np.float32).astype(dtype).astype(np.float64)
    return np.moveaxis((codes * scale).reshape(v.shape), -1, axis)


WIDE = False


def mx_kscale(k):
    if not WIDE:
        return np.ones(k)
    levels = np.array([10, -10, 5, -5, 0])
    a = np.random.permutation(np.resize(levels, k // 512 * 4)).reshape(k // 512, 4)
    idx = np.arange(k)
    return np.exp2(a[idx // 512, idx % 128 // 32])


BF16 = ml_dtypes.bfloat16


def bf(x):
    return np.asarray(x, np.float32).astype(BF16)


def f64(x):
    return np.asarray(x).astype(np.float64)


E2M1 = np.array([0.0, 0.5, 1.0, 1.5, 2.0, 3.0, 4.0, 6.0, -0.0, -0.5, -1.0, -1.5, -2.0, -3.0, -4.0, -6.0])


def pack_weight(w, fmt):
    k, n = w.shape
    w = f64(bf(w)).reshape(k // 32, 32, n)
    amax = np.abs(w).max(1)
    if fmt == "e4m3":
        byte = np.frexp(amax)[1] - 1 + 127 - 7
    else:
        mant, ex = np.frexp(amax / 6.0)
        byte = np.where(mant > 0.5, ex, ex - 1) + 127
    byte = np.clip(np.where(amax > 0, byte, 1), 1, 254)
    scaled = (w * np.exp2(127.0 - byte)[:, None, :]).reshape(k, n).astype(np.float32)
    by_word = np.ascontiguousarray(scaled.reshape(k // 512, 128, 4, n).transpose(0, 1, 3, 2))
    if fmt == "e4m3":
        words = by_word.astype(ml_dtypes.float8_e4m3fn).view(np.uint8)
    else:
        c = by_word.astype(ml_dtypes.float4_e2m1fn).view(np.uint8) & 0xF
        words = c[..., 0::2] | (c[..., 1::2] << 4)
    return np.ascontiguousarray(words), np.ascontiguousarray(byte.astype(np.uint8).reshape(k // 512, 16, n))


def unpack_weight(words, scales, fmt):
    g, p, n, _ = words.shape
    if fmt == "e4m3":
        vals = np.ascontiguousarray(words).view(ml_dtypes.float8_e4m3fn).astype(np.float64)
    else:
        nib = np.empty((g, p, n, 4), np.uint8)
        nib[..., 0::2] = words & 0xF
        nib[..., 1::2] = words >> 4
        vals = E2M1[nib]
    vals = vals * np.repeat(np.exp2(scales.astype(np.float64) - 127.0), 8, axis=1)[..., None]
    return vals.transpose(0, 1, 3, 2).reshape(g * 512, n)


B, N, D, C, H, NS = 2, 1024, 1024, 1024, 16, 10
HD = C // H
D4 = (0.4829629131445341, 0.8365163037378079, 0.2241438680420134, -0.1294095225512604)


def causal_multiscale(x_c, scale_gain):
    g = np.exp(scale_gain - scale_gain.max(0, keepdims=True))
    gains = g / g.sum(0, keepdims=True)
    gains_exp = np.repeat(gains, HD, axis=1)
    out = np.zeros_like(x_c)
    for j in range(NS):
        d = 2 ** j
        xp = np.pad(x_c, ((0, 0), (0, 0), (3 * d, 0)))
        y = (D4[0] * xp[:, :, 0 * d:0 * d + N]
             + D4[1] * xp[:, :, 1 * d:1 * d + N]
             + D4[2] * xp[:, :, 2 * d:2 * d + N]
             + D4[3] * xp[:, :, 3 * d:3 * d + N])
        out = out + gains_exp[j][None, :, None] * y
    return out


def setup_inputs():
    s = mx_kscale(D)
    x = bf(np.random.standard_normal((B, N, D)) * s)
    k_w = np.random.standard_normal((C, D)) / np.sqrt(D) / s[None, :]
    k_b = bf(np.random.standard_normal(C) * 0.2)
    v_w = np.random.standard_normal((C, D)) / np.sqrt(D) / s[None, :]
    v_b = bf(np.random.standard_normal(C) * 0.2)
    scale_gain = bf(np.random.standard_normal((NS, H)) * 0.5)
    k_w_words, k_w_scales = pack_weight(np.ascontiguousarray(k_w.T), "e4m3")
    v_w_words, v_w_scales = pack_weight(np.ascontiguousarray(v_w.T), "e4m3")
    return {"x": x,
            "k_w_words": k_w_words,
            "k_w_scales": k_w_scales,
            "k_b": k_b,
            "v_w_words": v_w_words,
            "v_w_scales": v_w_scales,
            "v_b": v_b,
            "scale_gain": scale_gain}


def reference(x, k_w_words, k_w_scales, k_b, v_w_words, v_w_scales, v_b, scale_gain):
    xq = mxq(f64(x), 2, "e4m3")
    k = ((xq @ unpack_weight(k_w_words, k_w_scales, "e4m3")) + f64(k_b)).reshape(B, N, H, HD)
    v = ((xq @ unpack_weight(v_w_words, v_w_scales, "e4m3")) + f64(v_b)).reshape(B, N, H, HD)
    k_mag = np.sqrt((k * k).sum(-1, keepdims=True))
    field = v * k_mag
    x_c = field.transpose(0, 2, 3, 1).reshape(B, C, N)
    return causal_multiscale(x_c, f64(scale_gain))

@@ -1,0 +1,219 @@
+from contextlib import ExitStack
+
+import concourse.mybir as mybir
+from concourse.masks import make_identity
+
+F32 = mybir.dt.float32
+BF16 = mybir.dt.bfloat16
+I32 = mybir.dt.int32
+U32 = mybir.dt.uint32
+U8 = mybir.dt.uint8
+FP8X4 = mybir.dt.float8_e4m3fn_x4
+ALU = mybir.AluOpType
+ACT = mybir.ActivationFunctionType
+AXIS_X = mybir.AxisListType.X
+
+P = 128
+BATCH, TOKENS, WIDTH, CHANNELS, HEADS, SCALES = 2, 1024, 1024, 1024, 16, 10
+HEAD_DIM = CHANNELS // HEADS
+ALL_TOKENS = BATCH * TOKENS
+K_PASS = 4 * P
+PASSES = WIDTH // K_PASS
+TOKEN_TILES = ALL_TOKENS // P
+CHANNEL_TILES = CHANNELS // P
+N_MOVING = 512
+TOKEN_GROUPS = ALL_TOKENS // N_MOVING
+GROUPS_PER_BATCH = TOKENS // N_MOVING
+T0, T1, T2, T3 = 0.4829629131445341, 0.8365163037378079, 0.2241438680420134, -0.1294095225512604
+
+FLOPS = 2 * ALL_TOKENS * WIDTH * 2 * CHANNELS
+
+
+def tile_causalwaveletfieldattentionbyte_pa_kernel(
+    tc, x, k_w_words, k_w_scales, k_b, v_w_words, v_w_scales, v_b, scale_gain, out
+):
+    nc = tc.nc
+    with ExitStack() as ctx:
+        keep = ctx.enter_context(tc.tile_pool(name="keep", bufs=1))
+        stage = ctx.enter_context(tc.tile_pool(name="stage", bufs=2))
+        psum_x = ctx.enter_context(tc.psum_pool(name="psum_x", bufs=2))
+        psum_k = ctx.enter_context(tc.psum_pool(name="psum_k", bufs=2))
+        psum_v = ctx.enter_context(tc.psum_pool(name="psum_v", bufs=2))
+        psum_m = ctx.enter_context(tc.psum_pool(name="psum_m", bufs=2))
+
+        w_planes = keep.tile([P, CHANNELS], U8, align_bytes=64)
+        nc.vector.memset(w_planes[:].bitcast(I32), 0)
+
+        x_sb = keep.tile([P, TOKEN_TILES, WIDTH], BF16)
+        x_rows = x.rearrange("b n d -> (b n) d").rearrange("(t p) d -> p t d", p=P)
+        tiles_per_load = TOKEN_TILES // TOKEN_GROUPS
+        nc.sync.dma_start(out=x_sb[:, 0:tiles_per_load, :], in_=x_rows[:, 0:tiles_per_load, :])
+
+        for w_index, scales in enumerate((k_w_scales, v_w_scales)):
+            for quadrant in range(4):
+                first = 32 * quadrant + 4 * PASSES * w_index
+                nc.sync.dma_start(
+                    out=w_planes[first : first + 4 * PASSES, :].bitcast(I32),
+                    in_=scales[:, 4 * quadrant : 4 * quadrant + 4, :].bitcast(I32),
+                )
+
+        k_words = keep.tile([P, PASSES, CHANNELS], U32, align_bytes=64)
+        v_words = keep.tile([P, PASSES, CHANNELS], U32, align_bytes=64)
+        nc.sync.dma_start(
+            out=k_words[:].bitcast(I32), in_=k_w_words.rearrange("g p n t -> p g (n t)").bitcast(I32)
+        )
+        nc.sync.dma_start(
+            out=v_words[:].bitcast(I32), in_=v_w_words.rearrange("g p n t -> p g (n t)").bitcast(I32)
+        )
+        for group in range(1, TOKEN_GROUPS):
+            tiles = slice(group * tiles_per_load, (group + 1) * tiles_per_load)
+            nc.sync.dma_start(out=x_sb[:, tiles, :], in_=x_rows[:, tiles, :])
+
+        gain_rows = keep.tile([P, SCALES * HEADS], BF16)
+        nc.scalar.dma_start(
+            out=gain_rows[:], in_=scale_gain.rearrange("j h -> (j h)").partition_broadcast(P)
+        )
+        bias_rows = keep.tile([P, P], BF16)
+        nc.vector.memset(bias_rows[:], 0.0)
+        nc.scalar.dma_start(
+            out=bias_rows[0:CHANNEL_TILES, :], in_=k_b.rearrange("(r c) -> r c", c=P)
+        )
+        nc.scalar.dma_start(
+            out=bias_rows[CHANNEL_TILES : 2 * CHANNEL_TILES, :], in_=v_b.rearrange("(r c) -> r c", c=P)
+        )
+
+        ident = keep.tile([P, P], F32)
+        make_identity(nc, ident[:])
+        same_head = keep.tile([P, P], F32)
+        nc.vector.memset(same_head[:], 0.0)
+        nc.vector.memset(same_head[0:HEAD_DIM, 0:HEAD_DIM], 1.0)
+        nc.vector.memset(same_head[HEAD_DIM:P, HEAD_DIM:P], 1.0)
+
+        bias_rows_f32 = keep.tile([P, P], F32)
+        nc.vector.tensor_copy(out=bias_rows_f32[:], in_=bias_rows[:])
+        bias_ps = psum_x.tile([P, P], F32, tag="xt")
+        nc.tensor.transpose(bias_ps[:], bias_rows_f32[:], ident[:])
+        bias = keep.tile([P, 2 * CHANNEL_TILES], F32)
+        nc.vector.tensor_copy(out=bias[:], in_=bias_ps[:, 0 : 2 * CHANNEL_TILES])
+
+        by_head = gain_rows[:].rearrange("p (j i two) -> p two i j", i=CHANNEL_TILES, two=2)
+        logit = keep.tile([P, CHANNEL_TILES, SCALES], F32)
+        nc.vector.tensor_copy(out=logit[0:HEAD_DIM], in_=by_head[0:HEAD_DIM, 0])
+        nc.vector.tensor_copy(out=logit[HEAD_DIM:P], in_=by_head[HEAD_DIM:P, 1])
+        gain_shape = [P, CHANNEL_TILES, SCALES]
+        top = keep.tile([P, CHANNEL_TILES], F32)
+        nc.vector.tensor_reduce(out=top[:], in_=logit[:], axis=AXIS_X, op=ALU.max)
+        nc.vector.tensor_tensor(
+            out=logit[:], in0=logit[:], in1=top[:].unsqueeze(2).to_broadcast(gain_shape), op=ALU.subtract
+        )
+        expd = keep.tile(gain_shape, F32)
+        nc.scalar.activation(out=expd[:], in_=logit[:], func=ACT.Exp)
+        total = keep.tile([P, CHANNEL_TILES], F32)
+        nc.vector.tensor_reduce(out=total[:], in_=expd[:], axis=AXIS_X, op=ALU.add)
+        inverse = keep.tile([P, CHANNEL_TILES], F32)
+        nc.vector.reciprocal(out=inverse[:], in_=total[:])
+        gain = keep.tile(gain_shape, F32)
+        nc.vector.tensor_tensor(
+            out=gain[:], in0=expd[:], in1=inverse[:].unsqueeze(2).to_broadcast(gain_shape), op=ALU.mult
+        )
+        w_pow2 = keep.tile(gain_shape, F32)
+        nc.vector.tensor_scalar_mul(out=w_pow2[:], in0=gain[:], scalar1=T2)
+        nc.vector.scalar_tensor_tensor(
+            out=w_pow2[:, :, 1:SCALES],
+            in0=gain[:, :, 0 : SCALES - 1],
+            scalar=T1,
+            in1=w_pow2[:, :, 1:SCALES],
+            op0=ALU.mult,
+            op1=ALU.add,
+        )
+        w_three = keep.tile(gain_shape, F32)
+        nc.vector.tensor_scalar_mul(out=w_three[:], in0=gain[:], scalar1=T0)
+
+        x_words = x_sb[:].bitcast(F32)
+        x_codes = keep.tile([P, PASSES, ALL_TOKENS], U32, align_bytes=64)
+        x_planes = keep.tile([P, PASSES, ALL_TOKENS], U8, align_bytes=64)
+        tokens_per_bank = 2 * P
+        for group in range(TOKEN_GROUPS):
+            for g in range(PASSES):
+                grouped = stage.tile([P, 4 * N_MOVING], BF16, align_bytes=64)
+                grouped_words = grouped[:].bitcast(F32).rearrange("p (n u) -> p n u", u=2)
+                for half in range(N_MOVING // tokens_per_bank):
+                    xt = psum_x.tile([P, 2, tokens_per_bank], F32, tag="xt")
+                    for u in range(2):
+                        for s in range(tokens_per_bank // P):
+                            t = group * tiles_per_load + half * (tokens_per_bank // P) + s
+                            nc.tensor.transpose(
+                                xt[:, u, s * P : (s + 1) * P],
+                                x_words[:, t, 256 * g + u : 256 * (g + 1) : 2],
+                                ident[:],
+                            )
+                    dst = grouped_words[:, half * tokens_per_bank : (half + 1) * tokens_per_bank, :]
+                    src = xt[:].rearrange("p u n -> p n u")
+                    if half == 0:
+                        nc.vector.tensor_copy(out=dst, in_=src)
+                    else:
+                        nc.scalar.copy(out=dst, in_=src)
+                cols = slice(group * N_MOVING, (group + 1) * N_MOVING)
+                nc.vector.quantize_mx(
+                    out=x_codes[:, g, cols].bitcast(FP8X4), scales=x_planes[:, g, cols], in_=grouped[:]
+                )
+
+        def project(acc, words, first_plane, channels, tokens):
+            for g in range(PASSES):
+                nc.tensor.matmul_mx(
+                    out=acc,
+                    lhsT=words[:, g, channels].bitcast(FP8X4),
+                    lhsT_scale=w_planes[4 * (first_plane + g) : P, channels],
+                    rhs=x_codes[:, g, tokens].bitcast(FP8X4),
+                    rhs_scale=x_planes[:, g, tokens],
+                    start=(g == 0),
+                    stop=(g == PASSES - 1),
+                )
+
+        distances = [(2**i, w_pow2, i) for i in range(SCALES)]
+        distances += [(3 * 2**j, w_three, j) for j in range(SCALES) if 3 * 2**j < TOKENS]
+
+        for i in range(CHANNEL_TILES):
+            channels = slice(i * P, (i + 1) * P)
+            field = stage.tile([P, BATCH, TOKENS], F32)
+            for b in range(BATCH):
+                for part in range(GROUPS_PER_BATCH):
+                    first = b * TOKENS + part * N_MOVING
+                    tokens = slice(first, first + N_MOVING)
+                    k_ps = psum_k.tile([P, N_MOVING], F32)
+                    project(k_ps[:], k_words, 0, channels, tokens)
+                    v_ps = psum_v.tile([P, N_MOVING], F32)
+                    project(v_ps[:], v_words, PASSES, channels, tokens)
+                    squares = stage.tile([P, N_MOVING], F32)
+                    nc.scalar.activation(
+                        out=squares[:], in_=k_ps[:], func=ACT.Square, bias=bias[:, i : i + 1]
+                    )
+                    norm2_ps = psum_m.tile([P, N_MOVING], F32)
+                    nc.tensor.matmul(
+                        out=norm2_ps[:], lhsT=same_head[:], rhs=squares[:], start=True, stop=True
+                    )
+                    norm = stage.tile([P, N_MOVING], F32)
+                    nc.scalar.activation(out=norm[:], in_=norm2_ps[:], func=ACT.Sqrt)
+                    nc.vector.scalar_tensor_tensor(
+                        out=field[:, b, part * N_MOVING : (part + 1) * N_MOVING],
+                        in0=v_ps[:],
+                        scalar=bias[:, CHANNEL_TILES + i : CHANNEL_TILES + i + 1],
+                        in1=norm[:],
+                        op0=ALU.add,
+                        op1=ALU.mult,
+                    )
+            result = stage.tile([P, BATCH, TOKENS], F32)
+            for b in range(BATCH):
+                nc.scalar.activation(out=result[:, b, :], in_=field[:, b, :], func=ACT.Copy, scale=T3)
+            for distance, weights, column in distances:
+                for b in range(BATCH):
+                    nc.vector.scalar_tensor_tensor(
+                        out=result[:, b, distance:TOKENS],
+                        in0=field[:, b, 0 : TOKENS - distance],
+                        scalar=weights[:, i, column : column + 1],
+                        in1=result[:, b, distance:TOKENS],
+                        op0=ALU.mult,
+                        op1=ALU.add,
+                    )
+            for b in range(BATCH):
+                nc.sync.dma_start(out=out[b, channels, :], in_=result[:, b, :])

@@ -19,11 +19,13 @@ HEAD_DIM = CHANNELS // HEADS
 ALL_TOKENS = BATCH * TOKENS
 K_PASS = 4 * P
 PASSES = WIDTH // K_PASS
-TOKEN_TILES = ALL_TOKENS // P
 CHANNEL_TILES = CHANNELS // P
-N_MOVING = 512
-TOKEN_GROUPS = ALL_TOKENS // N_MOVING
-GROUPS_PER_BATCH = TOKENS // N_MOVING
+BANK = 512
+RESIDUES = 4
+BLOCKS = TOKENS // (RESIDUES * P)
+RA = RESIDUES * BLOCKS
+TOKEN_TILES = RA * BATCH
+TILES_PER_BANK = BANK // P
 T0, T1, T2, T3 = 0.4829629131445341, 0.8365163037378079, 0.2241438680420134, -0.1294095225512604
 
 FLOPS = 2 * ALL_TOKENS * WIDTH * 2 * CHANNELS
@@ -36,19 +38,10 @@ def tile_causalwaveletfieldattentionbyte_pa_kernel(
     with ExitStack() as ctx:
         keep = ctx.enter_context(tc.tile_pool(name="keep", bufs=1))
         stage = ctx.enter_context(tc.tile_pool(name="stage", bufs=2))
-        psum_x = ctx.enter_context(tc.psum_pool(name="psum_x", bufs=2))
-        psum_k = ctx.enter_context(tc.psum_pool(name="psum_k", bufs=2))
-        psum_v = ctx.enter_context(tc.psum_pool(name="psum_v", bufs=2))
-        psum_m = ctx.enter_context(tc.psum_pool(name="psum_m", bufs=2))
+        psum_norm = ctx.enter_context(tc.psum_pool(name="psum_norm", bufs=2))
 
         w_planes = keep.tile([P, CHANNELS], U8, align_bytes=64)
         nc.vector.memset(w_planes[:].bitcast(I32), 0)
-
-        x_sb = keep.tile([P, TOKEN_TILES, WIDTH], BF16)
-        x_rows = x.rearrange("b n d -> (b n) d").rearrange("(t p) d -> p t d", p=P)
-        tiles_per_load = TOKEN_TILES // TOKEN_GROUPS
-        nc.sync.dma_start(out=x_sb[:, 0:tiles_per_load, :], in_=x_rows[:, 0:tiles_per_load, :])
-
         for w_index, scales in enumerate((k_w_scales, v_w_scales)):
             for quadrant in range(4):
                 first = 32 * quadrant + 4 * PASSES * w_index
@@ -57,65 +50,45 @@ def tile_causalwaveletfieldattentionbyte_pa_kernel(
                     in_=scales[:, 4 * quadrant : 4 * quadrant + 4, :].bitcast(I32),
                 )
 
-        k_words = keep.tile([P, PASSES, CHANNELS], U32, align_bytes=64)
-        v_words = keep.tile([P, PASSES, CHANNELS], U32, align_bytes=64)
-        nc.sync.dma_start(
-            out=k_words[:].bitcast(I32), in_=k_w_words.rearrange("g p n t -> p g (n t)").bitcast(I32)
-        )
-        nc.sync.dma_start(
-            out=v_words[:].bitcast(I32), in_=v_w_words.rearrange("g p n t -> p g (n t)").bitcast(I32)
-        )
-        for group in range(1, TOKEN_GROUPS):
-            tiles = slice(group * tiles_per_load, (group + 1) * tiles_per_load)
-            nc.sync.dma_start(out=x_sb[:, tiles, :], in_=x_rows[:, tiles, :])
-
         gain_rows = keep.tile([P, SCALES * HEADS], BF16)
         nc.scalar.dma_start(
             out=gain_rows[:], in_=scale_gain.rearrange("j h -> (j h)").partition_broadcast(P)
         )
-        bias_rows = keep.tile([P, P], BF16)
-        nc.vector.memset(bias_rows[:], 0.0)
+        k_bias_rows = keep.tile([P, P], BF16)
+        nc.vector.memset(k_bias_rows[:], 0.0)
         nc.scalar.dma_start(
-            out=bias_rows[0:CHANNEL_TILES, :], in_=k_b.rearrange("(r c) -> r c", c=P)
+            out=k_bias_rows[0:CHANNEL_TILES, :], in_=k_b.rearrange("(row c) -> row c", c=P)
         )
-        nc.scalar.dma_start(
-            out=bias_rows[CHANNEL_TILES : 2 * CHANNEL_TILES, :], in_=v_b.rearrange("(r c) -> r c", c=P)
-        )
+        v_bias = keep.tile([P, CHANNELS], BF16)
+        nc.scalar.dma_start(out=v_bias[:], in_=v_b.partition_broadcast(P))
 
         ident = keep.tile([P, P], F32)
         make_identity(nc, ident[:])
-        same_head = keep.tile([P, P], F32)
-        nc.vector.memset(same_head[:], 0.0)
-        nc.vector.memset(same_head[0:HEAD_DIM, 0:HEAD_DIM], 1.0)
-        nc.vector.memset(same_head[HEAD_DIM:P, HEAD_DIM:P], 1.0)
+        head_pick = keep.tile([P, 2], F32)
+        nc.vector.memset(head_pick[:], 0.0)
+        nc.vector.memset(head_pick[0:HEAD_DIM, 0:1], 1.0)
+        nc.vector.memset(head_pick[HEAD_DIM:P, 1:2], 1.0)
 
-        bias_rows_f32 = keep.tile([P, P], F32)
-        nc.vector.tensor_copy(out=bias_rows_f32[:], in_=bias_rows[:])
-        bias_ps = psum_x.tile([P, P], F32, tag="xt")
-        nc.tensor.transpose(bias_ps[:], bias_rows_f32[:], ident[:])
-        bias = keep.tile([P, 2 * CHANNEL_TILES], F32)
-        nc.vector.tensor_copy(out=bias[:], in_=bias_ps[:, 0 : 2 * CHANNEL_TILES])
-
-        by_head = gain_rows[:].rearrange("p (j i two) -> p two i j", i=CHANNEL_TILES, two=2)
-        logit = keep.tile([P, CHANNEL_TILES, SCALES], F32)
-        nc.vector.tensor_copy(out=logit[0:HEAD_DIM], in_=by_head[0:HEAD_DIM, 0])
-        nc.vector.tensor_copy(out=logit[HEAD_DIM:P], in_=by_head[HEAD_DIM:P, 1])
-        gain_shape = [P, CHANNEL_TILES, SCALES]
-        top = keep.tile([P, CHANNEL_TILES], F32)
+        gain_shape = [P, HEADS, SCALES]
+        logit = keep.tile(gain_shape, F32)
+        nc.vector.tensor_copy(out=logit[:], in_=gain_rows[:].rearrange("p (j h) -> p h j", h=HEADS))
+        top = keep.tile([P, HEADS], F32)
         nc.vector.tensor_reduce(out=top[:], in_=logit[:], axis=AXIS_X, op=ALU.max)
         nc.vector.tensor_tensor(
             out=logit[:], in0=logit[:], in1=top[:].unsqueeze(2).to_broadcast(gain_shape), op=ALU.subtract
         )
         expd = keep.tile(gain_shape, F32)
         nc.scalar.activation(out=expd[:], in_=logit[:], func=ACT.Exp)
-        total = keep.tile([P, CHANNEL_TILES], F32)
+        total = keep.tile([P, HEADS], F32)
         nc.vector.tensor_reduce(out=total[:], in_=expd[:], axis=AXIS_X, op=ALU.add)
-        inverse = keep.tile([P, CHANNEL_TILES], F32)
+        inverse = keep.tile([P, HEADS], F32)
         nc.vector.reciprocal(out=inverse[:], in_=total[:])
         gain = keep.tile(gain_shape, F32)
         nc.vector.tensor_tensor(
             out=gain[:], in0=expd[:], in1=inverse[:].unsqueeze(2).to_broadcast(gain_shape), op=ALU.mult
         )
+        gain_sum = keep.tile([P, HEADS], F32)
+        nc.vector.tensor_reduce(out=gain_sum[:], in_=gain[:], axis=AXIS_X, op=ALU.add)
         w_pow2 = keep.tile(gain_shape, F32)
         nc.vector.tensor_scalar_mul(out=w_pow2[:], in0=gain[:], scalar1=T2)
         nc.vector.scalar_tensor_tensor(
@@ -129,91 +102,218 @@ def tile_causalwaveletfieldattentionbyte_pa_kernel(
         w_three = keep.tile(gain_shape, F32)
         nc.vector.tensor_scalar_mul(out=w_three[:], in0=gain[:], scalar1=T0)
 
-        x_words = x_sb[:].bitcast(F32)
         x_codes = keep.tile([P, PASSES, ALL_TOKENS], U32, align_bytes=64)
         x_planes = keep.tile([P, PASSES, ALL_TOKENS], U8, align_bytes=64)
-        tokens_per_bank = 2 * P
-        for group in range(TOKEN_GROUPS):
-            for g in range(PASSES):
-                grouped = stage.tile([P, 4 * N_MOVING], BF16, align_bytes=64)
-                grouped_words = grouped[:].bitcast(F32).rearrange("p (n u) -> p n u", u=2)
-                for half in range(N_MOVING // tokens_per_bank):
-                    xt = psum_x.tile([P, 2, tokens_per_bank], F32, tag="xt")
-                    for u in range(2):
-                        for s in range(tokens_per_bank // P):
-                            t = group * tiles_per_load + half * (tokens_per_bank // P) + s
-                            nc.tensor.transpose(
-                                xt[:, u, s * P : (s + 1) * P],
-                                x_words[:, t, 256 * g + u : 256 * (g + 1) : 2],
-                                ident[:],
-                            )
-                    dst = grouped_words[:, half * tokens_per_bank : (half + 1) * tokens_per_bank, :]
-                    src = xt[:].rearrange("p u n -> p n u")
-                    if half == 0:
-                        nc.vector.tensor_copy(out=dst, in_=src)
-                    else:
-                        nc.scalar.copy(out=dst, in_=src)
-                cols = slice(group * N_MOVING, (group + 1) * N_MOVING)
-                nc.vector.quantize_mx(
-                    out=x_codes[:, g, cols].bitcast(FP8X4), scales=x_planes[:, g, cols], in_=grouped[:]
-                )
+        k_words = keep.tile([P, PASSES, CHANNELS], U32, align_bytes=64)
+        v_words = keep.tile([P, PASSES, CHANNELS], U32, align_bytes=64)
+        toeplitz = keep.tile([P, HEADS, 2 * P], F32)
+        field = keep.tile([P, RA, HEADS, BATCH, HEAD_DIM], F32)
+        norm = keep.tile([P, HEADS, TOKEN_TILES], F32)
 
-        def project(acc, words, first_plane, channels, tokens):
-            for g in range(PASSES):
-                nc.tensor.matmul_mx(
-                    out=acc,
-                    lhsT=words[:, g, channels].bitcast(FP8X4),
-                    lhsT_scale=w_planes[4 * (first_plane + g) : P, channels],
-                    rhs=x_codes[:, g, tokens].bitcast(FP8X4),
-                    rhs_scale=x_planes[:, g, tokens],
-                    start=(g == 0),
-                    stop=(g == PASSES - 1),
-                )
-
-        distances = [(2**i, w_pow2, i) for i in range(SCALES)]
-        distances += [(3 * 2**j, w_three, j) for j in range(SCALES) if 3 * 2**j < TOKENS]
-
-        for i in range(CHANNEL_TILES):
-            channels = slice(i * P, (i + 1) * P)
-            field = stage.tile([P, BATCH, TOKENS], F32)
-            for b in range(BATCH):
-                for part in range(GROUPS_PER_BATCH):
-                    first = b * TOKENS + part * N_MOVING
-                    tokens = slice(first, first + N_MOVING)
-                    k_ps = psum_k.tile([P, N_MOVING], F32)
-                    project(k_ps[:], k_words, 0, channels, tokens)
-                    v_ps = psum_v.tile([P, N_MOVING], F32)
-                    project(v_ps[:], v_words, PASSES, channels, tokens)
-                    squares = stage.tile([P, N_MOVING], F32)
-                    nc.scalar.activation(
-                        out=squares[:], in_=k_ps[:], func=ACT.Square, bias=bias[:, i : i + 1]
-                    )
-                    norm2_ps = psum_m.tile([P, N_MOVING], F32)
-                    nc.tensor.matmul(
-                        out=norm2_ps[:], lhsT=same_head[:], rhs=squares[:], start=True, stop=True
-                    )
-                    norm = stage.tile([P, N_MOVING], F32)
-                    nc.scalar.activation(out=norm[:], in_=norm2_ps[:], func=ACT.Sqrt)
-                    nc.vector.scalar_tensor_tensor(
-                        out=field[:, b, part * N_MOVING : (part + 1) * N_MOVING],
-                        in0=v_ps[:],
-                        scalar=bias[:, CHANNEL_TILES + i : CHANNEL_TILES + i + 1],
-                        in1=norm[:],
-                        op0=ALU.add,
-                        op1=ALU.mult,
-                    )
-            result = stage.tile([P, BATCH, TOKENS], F32)
-            for b in range(BATCH):
-                nc.scalar.activation(out=result[:, b, :], in_=field[:, b, :], func=ACT.Copy, scale=T3)
-            for distance, weights, column in distances:
+        with (
+            tc.tile_pool(name="early", bufs=1) as early,
+            tc.psum_pool(name="psum_front", bufs=2) as psum,
+        ):
+            x_sb = early.tile([P, RA, BATCH, WIDTH], BF16)
+            for r in range(RESIDUES):
                 for b in range(BATCH):
-                    nc.vector.scalar_tensor_tensor(
-                        out=result[:, b, distance:TOKENS],
-                        in0=field[:, b, 0 : TOKENS - distance],
-                        scalar=weights[:, i, column : column + 1],
-                        in1=result[:, b, distance:TOKENS],
-                        op0=ALU.mult,
-                        op1=ALU.add,
+                    nc.sync.dma_start(
+                        out=x_sb[:, BLOCKS * r : BLOCKS * (r + 1), b, :],
+                        in_=x[b].rearrange("(a i r) d -> r i a d", i=P, r=RESIDUES)[r],
                     )
-            for b in range(BATCH):
-                nc.sync.dma_start(out=out[b, channels, :], in_=result[:, b, :])
+                if r == 0:
+                    nc.sync.dma_start(
+                        out=v_words[:].bitcast(I32),
+                        in_=v_w_words.rearrange("g p n t -> p g (n t)").bitcast(I32),
+                    )
+            nc.sync.dma_start(
+                out=k_words[:].bitcast(I32), in_=k_w_words.rearrange("g p n t -> p g (n t)").bitcast(I32)
+            )
+
+            row_len = 3 * P
+            weight_row = early.tile([P, HEADS, row_len], F32)
+            nc.gpsimd.memset(weight_row[:], 0.0)
+            nc.vector.tensor_scalar_mul(
+                out=weight_row[:, :, P - 1 : P], in0=gain_sum[:].unsqueeze(2), scalar1=T3
+            )
+            for i in range(2, SCALES):
+                at = P - 1 + 2 ** (i - 2)
+                nc.vector.tensor_copy(out=weight_row[:, :, at : at + 1], in_=w_pow2[:, :, i : i + 1])
+            for j in range(2, SCALES - 1):
+                at = P - 1 + 3 * 2 ** (j - 2)
+                nc.vector.tensor_copy(out=weight_row[:, :, at : at + 1], in_=w_three[:, :, j : j + 1])
+            flat_out = out.rearrange("b c n -> (b c n)")
+            pitch = HEADS * row_len
+            nc.sync.dma_start(
+                out=flat_out[0 : P * pitch].rearrange("(p e) -> p e", p=P),
+                in_=weight_row[:].rearrange("p h e -> p (h e)"),
+            )
+            for h in range(HEADS):
+                start = h * row_len + P - 1
+                shifted = flat_out[start : start + P * (pitch - 1)].rearrange("(p e) -> p e", p=P)
+                nc.sync.dma_start(out=toeplitz[:, h, :], in_=shifted[:, 0 : 2 * P])
+
+            k_bias_rows_f32 = early.tile([P, P], F32)
+            nc.vector.tensor_copy(out=k_bias_rows_f32[:], in_=k_bias_rows[:])
+            k_bias_ps = psum.tile([P, P], F32, tag="xt")
+            nc.tensor.transpose(k_bias_ps[:], k_bias_rows_f32[:], ident[:])
+            k_bias = keep.tile([P, CHANNEL_TILES], F32)
+            nc.vector.tensor_copy(out=k_bias[:], in_=k_bias_ps[:, 0:CHANNEL_TILES])
+
+            x_words = x_sb[:].rearrange("p ra b d -> p (ra b) d").bitcast(F32)
+            tiles_per_xt = 2
+            for group in range(TOKEN_TILES // TILES_PER_BANK):
+                for g in range(PASSES):
+                    grouped = stage.tile([P, 4 * BANK], BF16, align_bytes=64)
+                    grouped_words = grouped[:].bitcast(F32).rearrange("p (n u) -> p n u", u=2)
+                    for half in range(TILES_PER_BANK // tiles_per_xt):
+                        xt = psum.tile([P, 2, tiles_per_xt * P], F32, tag="xt")
+                        for u in range(2):
+                            for s in range(tiles_per_xt):
+                                t = group * TILES_PER_BANK + half * tiles_per_xt + s
+                                nc.tensor.transpose(
+                                    xt[:, u, s * P : (s + 1) * P],
+                                    x_words[:, t, 256 * g + u : 256 * (g + 1) : 2],
+                                    ident[:],
+                                )
+                        tokens = slice(half * tiles_per_xt * P, (half + 1) * tiles_per_xt * P)
+                        if half == 0:
+                            nc.vector.tensor_copy(
+                                out=grouped_words[:, tokens, :], in_=xt[:].rearrange("p u n -> p n u")
+                            )
+                        else:
+                            nc.scalar.copy(
+                                out=grouped_words[:, tokens, :], in_=xt[:].rearrange("p u n -> p n u")
+                            )
+                    cols = slice(group * BANK, (group + 1) * BANK)
+                    nc.vector.quantize_mx(
+                        out=x_codes[:, g, cols].bitcast(FP8X4), scales=x_planes[:, g, cols], in_=grouped[:]
+                    )
+
+            for ra in range(RA):
+                for b in range(BATCH):
+                    tokens = slice((ra * BATCH + b) * P, (ra * BATCH + b + 1) * P)
+                    for half in range(CHANNELS // BANK):
+                        channels = slice(half * BANK, (half + 1) * BANK)
+                        heads = slice(half * (BANK // HEAD_DIM), (half + 1) * (BANK // HEAD_DIM))
+                        v_ps = psum.tile([P, BANK], F32)
+                        for g in range(PASSES):
+                            nc.tensor.matmul_mx(
+                                out=v_ps[:],
+                                lhsT=x_codes[:, g, tokens].bitcast(FP8X4),
+                                lhsT_scale=x_planes[:, g, tokens],
+                                rhs=v_words[:, g, channels].bitcast(FP8X4),
+                                rhs_scale=w_planes[4 * (PASSES + g) : P, channels],
+                                start=(g == 0),
+                                stop=(g == PASSES - 1),
+                            )
+                        nc.vector.tensor_tensor(
+                            out=field[:, ra, heads, b, :],
+                            in0=v_ps[:].rearrange("p (h c) -> p h c", c=HEAD_DIM),
+                            in1=v_bias[:, channels].rearrange("p (h c) -> p h c", c=HEAD_DIM),
+                            op=ALU.add,
+                        )
+
+        def finish_field(i):
+            channels = slice(i * P, (i + 1) * P)
+            norm2_ps = psum_norm.tile([P, TOKEN_TILES, 2], F32)
+            for group in range(TOKEN_TILES // TILES_PER_BANK):
+                tokens = slice(group * BANK, (group + 1) * BANK)
+                k_ps = psum_norm.tile([P, BANK], F32)
+                for g in range(PASSES):
+                    nc.tensor.matmul_mx(
+                        out=k_ps[:],
+                        lhsT=k_words[:, g, channels].bitcast(FP8X4),
+                        lhsT_scale=w_planes[4 * g : P, channels],
+                        rhs=x_codes[:, g, tokens].bitcast(FP8X4),
+                        rhs_scale=x_planes[:, g, tokens],
+                        start=(g == 0),
+                        stop=(g == PASSES - 1),
+                    )
+                squares = stage.tile([P, BANK], F32)
+                nc.scalar.activation(
+                    out=squares[:], in_=k_ps[:], func=ACT.Square, bias=k_bias[:, i : i + 1]
+                )
+                for s in range(TILES_PER_BANK):
+                    nc.tensor.matmul(
+                        out=norm2_ps[:, group * TILES_PER_BANK + s, :],
+                        lhsT=squares[:, s * P : (s + 1) * P],
+                        rhs=head_pick[:],
+                        start=True,
+                        stop=True,
+                    )
+            nc.scalar.activation(
+                out=norm[:, 2 * i : 2 * i + 2, :],
+                in_=norm2_ps[:].rearrange("p t e -> p e t"),
+                func=ACT.Sqrt,
+            )
+            for h in (2 * i, 2 * i + 1):
+                nc.vector.tensor_tensor(
+                    out=field[:, :, h, :, :],
+                    in0=field[:, :, h, :, :],
+                    in1=norm[:, h, :]
+                    .rearrange("p (ra b) -> p ra b", b=BATCH)
+                    .unsqueeze(3)
+                    .to_broadcast([P, RA, BATCH, HEAD_DIM]),
+                    op=ALU.mult,
+                )
+
+        with (
+            tc.tile_pool(name="late", bufs=4) as late,
+            tc.psum_pool(name="psum_filter", bufs=1) as psum,
+        ):
+
+            def multiples_of_four(h):
+                sums_0 = psum.tile([P, RESIDUES, P], F32)
+                sums_1 = psum.tile([P, RESIDUES, P], F32)
+                turned_0 = psum.tile([P, RESIDUES, P], F32)
+                turned_1 = psum.tile([P, RESIDUES, P], F32)
+                near = toeplitz[:, h, 0:P]
+                far = toeplitz[:, h, P : 2 * P]
+                block_0 = [field[:, BLOCKS * r, h].rearrange("p b c -> p (b c)") for r in range(RESIDUES)]
+                block_1 = [field[:, BLOCKS * r + 1, h].rearrange("p b c -> p (b c)") for r in range(RESIDUES)]
+                for r in range(RESIDUES):
+                    nc.tensor.matmul(out=sums_0[:, r, :], lhsT=block_0[r], rhs=near, start=True, stop=True)
+                for r in range(RESIDUES):
+                    nc.tensor.matmul(out=sums_1[:, r, :], lhsT=block_0[r], rhs=far, start=True, stop=False)
+                    nc.tensor.matmul(out=sums_1[:, r, :], lhsT=block_1[r], rhs=near, start=False, stop=True)
+                for r in range(RESIDUES):
+                    nc.tensor.transpose(turned_0[:, r, :], block_0[r], ident[:])
+                for r in range(RESIDUES):
+                    nc.tensor.transpose(turned_1[:, r, :], block_1[r], ident[:])
+                result = late.tile([P, TOKENS], F32)
+                field_t = late.tile([P, TOKENS], F32)
+                for bank, natural, a in (
+                    (sums_0, result, 0),
+                    (sums_1, result, 1),
+                    (turned_0, field_t, 0),
+                    (turned_1, field_t, 1),
+                ):
+                    nc.scalar.copy(
+                        out=natural[:, a * BANK : (a + 1) * BANK].rearrange("p (i r) -> p i r", r=RESIDUES),
+                        in_=bank[:].rearrange("p r i -> p i r"),
+                    )
+                return h, field_t, result
+
+            short_distances = ((1, w_pow2, 0), (2, w_pow2, 1), (3, w_three, 0), (6, w_three, 1))
+            finish_field(0)
+            for pair in range(CHANNEL_TILES):
+                if pair + 1 < CHANNEL_TILES:
+                    finish_field(pair + 1)
+                two_heads = (multiples_of_four(2 * pair), multiples_of_four(2 * pair + 1))
+                for distance, weights, column in short_distances:
+                    for h, field_t, result in two_heads:
+                        nc.vector.scalar_tensor_tensor(
+                            out=result[:, distance:TOKENS],
+                            in0=field_t[:, 0 : TOKENS - distance],
+                            scalar=weights[:, h, column : column + 1],
+                            in1=result[:, distance:TOKENS],
+                            op0=ALU.mult,
+                            op1=ALU.add,
+                        )
+                for h, field_t, result in two_heads:
+                    for b in range(BATCH):
+                        nc.sync.dma_start(
+                            out=out[b, h * HEAD_DIM : (h + 1) * HEAD_DIM, :],
+                            in_=result[b * HEAD_DIM : (b + 1) * HEAD_DIM, :],
+                        )

@@ -19,7 +19,6 @@ HEAD_DIM = CHANNELS // HEADS
 ALL_TOKENS = BATCH * TOKENS
 K_PASS = 4 * P
 PASSES = WIDTH // K_PASS
-CHANNEL_TILES = CHANNELS // P
 BANK = 512
 RESIDUES = 4
 BLOCKS = TOKENS // (RESIDUES * P)
@@ -37,8 +36,6 @@ def tile_causalwaveletfieldattentionbyte_pa_kernel(
     nc = tc.nc
     with ExitStack() as ctx:
         keep = ctx.enter_context(tc.tile_pool(name="keep", bufs=1))
-        stage = ctx.enter_context(tc.tile_pool(name="stage", bufs=2))
-        psum_norm = ctx.enter_context(tc.psum_pool(name="psum_norm", bufs=2))
 
         w_planes = keep.tile([P, CHANNELS], U8, align_bytes=64)
         nc.vector.memset(w_planes[:].bitcast(I32), 0)
@@ -54,53 +51,13 @@ def tile_causalwaveletfieldattentionbyte_pa_kernel(
         nc.scalar.dma_start(
             out=gain_rows[:], in_=scale_gain.rearrange("j h -> (j h)").partition_broadcast(P)
         )
-        k_bias_rows = keep.tile([P, P], BF16)
-        nc.vector.memset(k_bias_rows[:], 0.0)
-        nc.scalar.dma_start(
-            out=k_bias_rows[0:CHANNEL_TILES, :], in_=k_b.rearrange("(row c) -> row c", c=P)
-        )
+        k_bias = keep.tile([P, CHANNELS], BF16)
+        nc.scalar.dma_start(out=k_bias[:], in_=k_b.partition_broadcast(P))
         v_bias = keep.tile([P, CHANNELS], BF16)
         nc.scalar.dma_start(out=v_bias[:], in_=v_b.partition_broadcast(P))
 
         ident = keep.tile([P, P], F32)
         make_identity(nc, ident[:])
-        head_pick = keep.tile([P, 2], F32)
-        nc.vector.memset(head_pick[:], 0.0)
-        nc.vector.memset(head_pick[0:HEAD_DIM, 0:1], 1.0)
-        nc.vector.memset(head_pick[HEAD_DIM:P, 1:2], 1.0)
-
-        gain_shape = [P, HEADS, SCALES]
-        logit = keep.tile(gain_shape, F32)
-        nc.vector.tensor_copy(out=logit[:], in_=gain_rows[:].rearrange("p (j h) -> p h j", h=HEADS))
-        top = keep.tile([P, HEADS], F32)
-        nc.vector.tensor_reduce(out=top[:], in_=logit[:], axis=AXIS_X, op=ALU.max)
-        nc.vector.tensor_tensor(
-            out=logit[:], in0=logit[:], in1=top[:].unsqueeze(2).to_broadcast(gain_shape), op=ALU.subtract
-        )
-        expd = keep.tile(gain_shape, F32)
-        nc.scalar.activation(out=expd[:], in_=logit[:], func=ACT.Exp)
-        total = keep.tile([P, HEADS], F32)
-        nc.vector.tensor_reduce(out=total[:], in_=expd[:], axis=AXIS_X, op=ALU.add)
-        inverse = keep.tile([P, HEADS], F32)
-        nc.vector.reciprocal(out=inverse[:], in_=total[:])
-        gain = keep.tile(gain_shape, F32)
-        nc.vector.tensor_tensor(
-            out=gain[:], in0=expd[:], in1=inverse[:].unsqueeze(2).to_broadcast(gain_shape), op=ALU.mult
-        )
-        gain_sum = keep.tile([P, HEADS], F32)
-        nc.vector.tensor_reduce(out=gain_sum[:], in_=gain[:], axis=AXIS_X, op=ALU.add)
-        w_pow2 = keep.tile(gain_shape, F32)
-        nc.vector.tensor_scalar_mul(out=w_pow2[:], in0=gain[:], scalar1=T2)
-        nc.vector.scalar_tensor_tensor(
-            out=w_pow2[:, :, 1:SCALES],
-            in0=gain[:, :, 0 : SCALES - 1],
-            scalar=T1,
-            in1=w_pow2[:, :, 1:SCALES],
-            op0=ALU.mult,
-            op1=ALU.add,
-        )
-        w_three = keep.tile(gain_shape, F32)
-        nc.vector.tensor_scalar_mul(out=w_three[:], in0=gain[:], scalar1=T0)
 
         x_codes = keep.tile([P, PASSES, ALL_TOKENS], U32, align_bytes=64)
         x_planes = keep.tile([P, PASSES, ALL_TOKENS], U8, align_bytes=64)
@@ -108,11 +65,17 @@ def tile_causalwaveletfieldattentionbyte_pa_kernel(
         v_words = keep.tile([P, PASSES, CHANNELS], U32, align_bytes=64)
         toeplitz = keep.tile([P, HEADS, 2 * P], F32)
         field = keep.tile([P, RA, HEADS, BATCH, HEAD_DIM], F32)
-        norm = keep.tile([P, HEADS, TOKEN_TILES], F32)
+        norm2 = keep.tile([P, TOKEN_TILES, HEADS], F32)
+        norm = keep.tile([P, TOKEN_TILES, HEADS], F32)
+        gain_shape = [P, HEADS, SCALES]
+        w_pow2 = keep.tile(gain_shape, F32)
+        w_three = keep.tile(gain_shape, F32)
 
         with (
             tc.tile_pool(name="early", bufs=1) as early,
-            tc.psum_pool(name="psum_front", bufs=2) as psum,
+            tc.tile_pool(name="stage", bufs=3) as stage,
+            tc.psum_pool(name="psum_front", bufs=2) as psum_x,
+            tc.psum_pool(name="psum_proj", bufs=3) as psum,
         ):
             x_sb = early.tile([P, RA, BATCH, WIDTH], BF16)
             for r in range(RESIDUES):
@@ -122,13 +85,47 @@ def tile_causalwaveletfieldattentionbyte_pa_kernel(
                         in_=x[b].rearrange("(a i r) d -> r i a d", i=P, r=RESIDUES)[r],
                     )
                 if r == 0:
-                    nc.sync.dma_start(
-                        out=v_words[:].bitcast(I32),
-                        in_=v_w_words.rearrange("g p n t -> p g (n t)").bitcast(I32),
-                    )
-            nc.sync.dma_start(
-                out=k_words[:].bitcast(I32), in_=k_w_words.rearrange("g p n t -> p g (n t)").bitcast(I32)
+                    for words, packed in ((k_words, k_w_words), (v_words, v_w_words)):
+                        nc.sync.dma_start(
+                            out=words[:].bitcast(I32),
+                            in_=packed.rearrange("g p n t -> p g (n t)").bitcast(I32),
+                        )
+
+            logit = early.tile(gain_shape, F32)
+            nc.vector.tensor_copy(out=logit[:], in_=gain_rows[:].rearrange("p (j h) -> p h j", h=HEADS))
+            top = early.tile([P, HEADS], F32)
+            nc.vector.tensor_reduce(out=top[:], in_=logit[:], axis=AXIS_X, op=ALU.max)
+            nc.vector.tensor_tensor(
+                out=logit[:],
+                in0=logit[:],
+                in1=top[:].unsqueeze(2).to_broadcast(gain_shape),
+                op=ALU.subtract,
             )
+            expd = early.tile(gain_shape, F32)
+            nc.scalar.activation(out=expd[:], in_=logit[:], func=ACT.Exp)
+            total = early.tile([P, HEADS], F32)
+            nc.vector.tensor_reduce(out=total[:], in_=expd[:], axis=AXIS_X, op=ALU.add)
+            inverse = early.tile([P, HEADS], F32)
+            nc.vector.reciprocal(out=inverse[:], in_=total[:])
+            gain = early.tile(gain_shape, F32)
+            nc.vector.tensor_tensor(
+                out=gain[:],
+                in0=expd[:],
+                in1=inverse[:].unsqueeze(2).to_broadcast(gain_shape),
+                op=ALU.mult,
+            )
+            gain_sum = early.tile([P, HEADS], F32)
+            nc.vector.tensor_reduce(out=gain_sum[:], in_=gain[:], axis=AXIS_X, op=ALU.add)
+            nc.vector.tensor_scalar_mul(out=w_pow2[:], in0=gain[:], scalar1=T2)
+            nc.vector.scalar_tensor_tensor(
+                out=w_pow2[:, :, 1:SCALES],
+                in0=gain[:, :, 0 : SCALES - 1],
+                scalar=T1,
+                in1=w_pow2[:, :, 1:SCALES],
+                op0=ALU.mult,
+                op1=ALU.add,
+            )
+            nc.vector.tensor_scalar_mul(out=w_three[:], in0=gain[:], scalar1=T0)
 
             row_len = 3 * P
             weight_row = early.tile([P, HEADS, row_len], F32)
@@ -153,13 +150,6 @@ def tile_causalwaveletfieldattentionbyte_pa_kernel(
                 shifted = flat_out[start : start + P * (pitch - 1)].rearrange("(p e) -> p e", p=P)
                 nc.sync.dma_start(out=toeplitz[:, h, :], in_=shifted[:, 0 : 2 * P])
 
-            k_bias_rows_f32 = early.tile([P, P], F32)
-            nc.vector.tensor_copy(out=k_bias_rows_f32[:], in_=k_bias_rows[:])
-            k_bias_ps = psum.tile([P, P], F32, tag="xt")
-            nc.tensor.transpose(k_bias_ps[:], k_bias_rows_f32[:], ident[:])
-            k_bias = keep.tile([P, CHANNEL_TILES], F32)
-            nc.vector.tensor_copy(out=k_bias[:], in_=k_bias_ps[:, 0:CHANNEL_TILES])
-
             x_words = x_sb[:].rearrange("p ra b d -> p (ra b) d").bitcast(F32)
             tiles_per_xt = 2
             for group in range(TOKEN_TILES // TILES_PER_BANK):
@@ -167,7 +157,7 @@ def tile_causalwaveletfieldattentionbyte_pa_kernel(
                     grouped = stage.tile([P, 4 * BANK], BF16, align_bytes=64)
                     grouped_words = grouped[:].bitcast(F32).rearrange("p (n u) -> p n u", u=2)
                     for half in range(TILES_PER_BANK // tiles_per_xt):
-                        xt = psum.tile([P, 2, tiles_per_xt * P], F32, tag="xt")
+                        xt = psum_x.tile([P, 2, tiles_per_xt * P], F32)
                         for u in range(2):
                             for s in range(tiles_per_xt):
                                 t = group * TILES_PER_BANK + half * tiles_per_xt + s
@@ -177,90 +167,67 @@ def tile_causalwaveletfieldattentionbyte_pa_kernel(
                                     ident[:],
                                 )
                         tokens = slice(half * tiles_per_xt * P, (half + 1) * tiles_per_xt * P)
-                        if half == 0:
-                            nc.vector.tensor_copy(
-                                out=grouped_words[:, tokens, :], in_=xt[:].rearrange("p u n -> p n u")
-                            )
-                        else:
-                            nc.scalar.copy(
-                                out=grouped_words[:, tokens, :], in_=xt[:].rearrange("p u n -> p n u")
-                            )
+                        nc.scalar.copy(
+                            out=grouped_words[:, tokens, :], in_=xt[:].rearrange("p u n -> p n u")
+                        )
                     cols = slice(group * BANK, (group + 1) * BANK)
                     nc.vector.quantize_mx(
                         out=x_codes[:, g, cols].bitcast(FP8X4), scales=x_planes[:, g, cols], in_=grouped[:]
                     )
 
-            for ra in range(RA):
-                for b in range(BATCH):
-                    tokens = slice((ra * BATCH + b) * P, (ra * BATCH + b + 1) * P)
-                    for half in range(CHANNELS // BANK):
-                        channels = slice(half * BANK, (half + 1) * BANK)
-                        heads = slice(half * (BANK // HEAD_DIM), (half + 1) * (BANK // HEAD_DIM))
-                        v_ps = psum.tile([P, BANK], F32)
-                        for g in range(PASSES):
-                            nc.tensor.matmul_mx(
-                                out=v_ps[:],
-                                lhsT=x_codes[:, g, tokens].bitcast(FP8X4),
-                                lhsT_scale=x_planes[:, g, tokens],
-                                rhs=v_words[:, g, channels].bitcast(FP8X4),
-                                rhs_scale=w_planes[4 * (PASSES + g) : P, channels],
-                                start=(g == 0),
-                                stop=(g == PASSES - 1),
-                            )
-                        nc.vector.tensor_tensor(
-                            out=field[:, ra, heads, b, :],
-                            in0=v_ps[:].rearrange("p (h c) -> p h c", c=HEAD_DIM),
-                            in1=v_bias[:, channels].rearrange("p (h c) -> p h c", c=HEAD_DIM),
-                            op=ALU.add,
-                        )
-
-        def finish_field(i):
-            channels = slice(i * P, (i + 1) * P)
-            norm2_ps = psum_norm.tile([P, TOKEN_TILES, 2], F32)
-            for group in range(TOKEN_TILES // TILES_PER_BANK):
-                tokens = slice(group * BANK, (group + 1) * BANK)
-                k_ps = psum_norm.tile([P, BANK], F32)
+            def project(acc, t, words, first_plane, channels):
+                tokens = slice(t * P, (t + 1) * P)
                 for g in range(PASSES):
                     nc.tensor.matmul_mx(
-                        out=k_ps[:],
-                        lhsT=k_words[:, g, channels].bitcast(FP8X4),
-                        lhsT_scale=w_planes[4 * g : P, channels],
-                        rhs=x_codes[:, g, tokens].bitcast(FP8X4),
-                        rhs_scale=x_planes[:, g, tokens],
+                        out=acc,
+                        lhsT=x_codes[:, g, tokens].bitcast(FP8X4),
+                        lhsT_scale=x_planes[:, g, tokens],
+                        rhs=words[:, g, channels].bitcast(FP8X4),
+                        rhs_scale=w_planes[4 * (first_plane + g) : P, channels],
                         start=(g == 0),
                         stop=(g == PASSES - 1),
                     )
-                squares = stage.tile([P, BANK], F32)
-                nc.scalar.activation(
-                    out=squares[:], in_=k_ps[:], func=ACT.Square, bias=k_bias[:, i : i + 1]
-                )
-                for s in range(TILES_PER_BANK):
-                    nc.tensor.matmul(
-                        out=norm2_ps[:, group * TILES_PER_BANK + s, :],
-                        lhsT=squares[:, s * P : (s + 1) * P],
-                        rhs=head_pick[:],
-                        start=True,
-                        stop=True,
+
+            heads_per_bank = BANK // HEAD_DIM
+            for t in range(TOKEN_TILES):
+                ra, b = divmod(t, BATCH)
+                for half in range(CHANNELS // BANK):
+                    channels = slice(half * BANK, (half + 1) * BANK)
+                    k_ps = psum.tile([P, BANK], F32)
+                    project(k_ps[:], t, k_words, 0, channels)
+                    k_biased = stage.tile([P, BANK], F32)
+                    nc.vector.tensor_tensor(out=k_biased[:], in0=k_ps[:], in1=k_bias[:, channels], op=ALU.add)
+                    squares = stage.tile([P, BANK], F32)
+                    for e in range(heads_per_bank):
+                        h = half * heads_per_bank + e
+                        nc.scalar.activation(
+                            out=squares[:, e * HEAD_DIM : (e + 1) * HEAD_DIM],
+                            in_=k_biased[:, e * HEAD_DIM : (e + 1) * HEAD_DIM],
+                            func=ACT.Square,
+                            accum_out=norm2[:, t, h : h + 1],
+                        )
+                for half in range(CHANNELS // BANK):
+                    channels = slice(half * BANK, (half + 1) * BANK)
+                    heads = slice(half * heads_per_bank, (half + 1) * heads_per_bank)
+                    v_ps = psum.tile([P, BANK], F32)
+                    project(v_ps[:], t, v_words, PASSES, channels)
+                    nc.vector.tensor_tensor(
+                        out=field[:, ra, heads, b, :],
+                        in0=v_ps[:].rearrange("p (h c) -> p h c", c=HEAD_DIM),
+                        in1=v_bias[:, channels].rearrange("p (h c) -> p h c", c=HEAD_DIM),
+                        op=ALU.add,
                     )
-            nc.scalar.activation(
-                out=norm[:, 2 * i : 2 * i + 2, :],
-                in_=norm2_ps[:].rearrange("p t e -> p e t"),
-                func=ACT.Sqrt,
-            )
-            for h in (2 * i, 2 * i + 1):
-                nc.vector.tensor_tensor(
-                    out=field[:, :, h, :, :],
-                    in0=field[:, :, h, :, :],
-                    in1=norm[:, h, :]
-                    .rearrange("p (ra b) -> p ra b", b=BATCH)
-                    .unsqueeze(3)
-                    .to_broadcast([P, RA, BATCH, HEAD_DIM]),
+                nc.scalar.activation(out=norm[:, t, :], in_=norm2[:, t, :], func=ACT.Sqrt)
+                nc.gpsimd.tensor_tensor(
+                    out=field[:, ra, :, b, :],
+                    in0=field[:, ra, :, b, :],
+                    in1=norm[:, t, :].unsqueeze(2).to_broadcast([P, HEADS, HEAD_DIM]),
                     op=ALU.mult,
                 )
 
         with (
             tc.tile_pool(name="late", bufs=4) as late,
-            tc.psum_pool(name="psum_filter", bufs=1) as psum,
+            tc.psum_pool(name="psum_filter", bufs=2) as psum,
         ):
 
             def multiples_of_four(h):
@@ -296,10 +263,7 @@ def tile_causalwaveletfieldattentionbyte_pa_kernel(
                 return h, field_t, result
 
             short_distances = ((1, w_pow2, 0), (2, w_pow2, 1), (3, w_three, 0), (6, w_three, 1))
-            finish_field(0)
-            for pair in range(CHANNEL_TILES):
-                if pair + 1 < CHANNEL_TILES:
-                    finish_field(pair + 1)
+            for pair in range(HEADS // 2):
                 two_heads = (multiples_of_four(2 * pair), multiples_of_four(2 * pair + 1))
                 for distance, weights, column in short_distances:
                     for h, field_t, result in two_heads:

@@ -36,6 +36,9 @@ def tile_causalwaveletfieldattentionbyte_pa_kernel(
     nc = tc.nc
     with ExitStack() as ctx:
         keep = ctx.enter_context(tc.tile_pool(name="keep", bufs=1))
+        stage = ctx.enter_context(tc.tile_pool(name="stage", bufs=3))
+        psum_proj = ctx.enter_context(tc.psum_pool(name="psum_proj", bufs=4))
+        psum_filter = ctx.enter_context(tc.psum_pool(name="psum_filter", bufs=1))
 
         w_planes = keep.tile([P, CHANNELS], U8, align_bytes=64)
         nc.vector.memset(w_planes[:].bitcast(I32), 0)
@@ -73,9 +76,7 @@ def tile_causalwaveletfieldattentionbyte_pa_kernel(
 
         with (
             tc.tile_pool(name="early", bufs=1) as early,
-            tc.tile_pool(name="stage", bufs=3) as stage,
-            tc.psum_pool(name="psum_front", bufs=2) as psum_x,
-            tc.psum_pool(name="psum_proj", bufs=3) as psum,
+            tc.tile_pool(name="regroup", bufs=3) as regroup,
         ):
             x_sb = early.tile([P, RA, BATCH, WIDTH], BF16)
             for r in range(RESIDUES):
@@ -154,10 +155,10 @@ def tile_causalwaveletfieldattentionbyte_pa_kernel(
             tiles_per_xt = 2
             for group in range(TOKEN_TILES // TILES_PER_BANK):
                 for g in range(PASSES):
-                    grouped = stage.tile([P, 4 * BANK], BF16, align_bytes=64)
+                    grouped = regroup.tile([P, 4 * BANK], BF16, align_bytes=64)
                     grouped_words = grouped[:].bitcast(F32).rearrange("p (n u) -> p n u", u=2)
                     for half in range(TILES_PER_BANK // tiles_per_xt):
-                        xt = psum_x.tile([P, 2, tiles_per_xt * P], F32)
+                        xt = psum_proj.tile([P, 2, tiles_per_xt * P], F32, tag="proj")
                         for u in range(2):
                             for s in range(tiles_per_xt):
                                 t = group * TILES_PER_BANK + half * tiles_per_xt + s
@@ -175,66 +176,61 @@ def tile_causalwaveletfieldattentionbyte_pa_kernel(
                         out=x_codes[:, g, cols].bitcast(FP8X4), scales=x_planes[:, g, cols], in_=grouped[:]
                     )
 
-            def project(acc, t, words, first_plane, channels):
-                tokens = slice(t * P, (t + 1) * P)
-                for g in range(PASSES):
-                    nc.tensor.matmul_mx(
-                        out=acc,
-                        lhsT=x_codes[:, g, tokens].bitcast(FP8X4),
-                        lhsT_scale=x_planes[:, g, tokens],
-                        rhs=words[:, g, channels].bitcast(FP8X4),
-                        rhs_scale=w_planes[4 * (first_plane + g) : P, channels],
-                        start=(g == 0),
-                        stop=(g == PASSES - 1),
-                    )
-
-            heads_per_bank = BANK // HEAD_DIM
-            for t in range(TOKEN_TILES):
-                ra, b = divmod(t, BATCH)
-                for half in range(CHANNELS // BANK):
-                    channels = slice(half * BANK, (half + 1) * BANK)
-                    k_ps = psum.tile([P, BANK], F32)
-                    project(k_ps[:], t, k_words, 0, channels)
-                    k_biased = stage.tile([P, BANK], F32)
-                    nc.vector.tensor_tensor(out=k_biased[:], in0=k_ps[:], in1=k_bias[:, channels], op=ALU.add)
-                    squares = stage.tile([P, BANK], F32)
-                    for e in range(heads_per_bank):
-                        h = half * heads_per_bank + e
-                        nc.scalar.activation(
-                            out=squares[:, e * HEAD_DIM : (e + 1) * HEAD_DIM],
-                            in_=k_biased[:, e * HEAD_DIM : (e + 1) * HEAD_DIM],
-                            func=ACT.Square,
-                            accum_out=norm2[:, t, h : h + 1],
-                        )
-                for half in range(CHANNELS // BANK):
-                    channels = slice(half * BANK, (half + 1) * BANK)
-                    heads = slice(half * heads_per_bank, (half + 1) * heads_per_bank)
-                    v_ps = psum.tile([P, BANK], F32)
-                    project(v_ps[:], t, v_words, PASSES, channels)
-                    nc.vector.tensor_tensor(
-                        out=field[:, ra, heads, b, :],
-                        in0=v_ps[:].rearrange("p (h c) -> p h c", c=HEAD_DIM),
-                        in1=v_bias[:, channels].rearrange("p (h c) -> p h c", c=HEAD_DIM),
-                        op=ALU.add,
-                    )
-                nc.scalar.activation(out=norm[:, t, :], in_=norm2[:, t, :], func=ACT.Sqrt)
-                nc.gpsimd.tensor_tensor(
-                    out=field[:, ra, :, b, :],
-                    in0=field[:, ra, :, b, :],
-                    in1=norm[:, t, :].unsqueeze(2).to_broadcast([P, HEADS, HEAD_DIM]),
-                    op=ALU.mult,
+        def project(t, words, first_plane, channels):
+            acc = psum_proj.tile([P, BANK], F32, tag="proj")
+            tokens = slice(t * P, (t + 1) * P)
+            for g in range(PASSES):
+                nc.tensor.matmul_mx(
+                    out=acc[:],
+                    lhsT=x_codes[:, g, tokens].bitcast(FP8X4),
+                    lhsT_scale=x_planes[:, g, tokens],
+                    rhs=words[:, g, channels].bitcast(FP8X4),
+                    rhs_scale=w_planes[4 * (first_plane + g) : P, channels],
+                    start=(g == 0),
+                    stop=(g == PASSES - 1),
                 )
+            return acc
 
-        with (
-            tc.tile_pool(name="late", bufs=4) as late,
-            tc.psum_pool(name="psum_filter", bufs=2) as psum,
-        ):
+        heads_per_bank = BANK // HEAD_DIM
+
+        def field_of(t, half):
+            ra, b = divmod(t, BATCH)
+            channels = slice(half * BANK, (half + 1) * BANK)
+            heads = slice(half * heads_per_bank, (half + 1) * heads_per_bank)
+            k_ps = project(t, k_words, 0, channels)
+            k_biased = stage.tile([P, BANK], F32)
+            nc.vector.tensor_tensor(out=k_biased[:], in0=k_ps[:], in1=k_bias[:, channels], op=ALU.add)
+            squares = stage.tile([P, BANK], F32)
+            for e in range(heads_per_bank):
+                h = half * heads_per_bank + e
+                nc.scalar.activation(
+                    out=squares[:, e * HEAD_DIM : (e + 1) * HEAD_DIM],
+                    in_=k_biased[:, e * HEAD_DIM : (e + 1) * HEAD_DIM],
+                    func=ACT.Square,
+                    accum_out=norm2[:, t, h : h + 1],
+                )
+            nc.scalar.activation(out=norm[:, t, heads], in_=norm2[:, t, heads], func=ACT.Sqrt)
+            v_ps = project(t, v_words, PASSES, channels)
+            nc.vector.tensor_tensor(
+                out=field[:, ra, heads, b, :],
+                in0=v_ps[:].rearrange("p (h c) -> p h c", c=HEAD_DIM),
+                in1=v_bias[:, channels].rearrange("p (h c) -> p h c", c=HEAD_DIM),
+                op=ALU.add,
+            )
+            nc.gpsimd.tensor_tensor(
+                out=field[:, ra, heads, b, :],
+                in0=field[:, ra, heads, b, :],
+                in1=norm[:, t, heads].unsqueeze(2).to_broadcast([P, heads_per_bank, HEAD_DIM]),
+                op=ALU.mult,
+            )
+
+        with tc.tile_pool(name="late", bufs=4) as late:
 
             def multiples_of_four(h):
-                sums_0 = psum.tile([P, RESIDUES, P], F32)
-                sums_1 = psum.tile([P, RESIDUES, P], F32)
-                turned_0 = psum.tile([P, RESIDUES, P], F32)
-                turned_1 = psum.tile([P, RESIDUES, P], F32)
+                sums_0 = psum_filter.tile([P, RESIDUES, P], F32)
+                sums_1 = psum_filter.tile([P, RESIDUES, P], F32)
+                turned_0 = psum_filter.tile([P, RESIDUES, P], F32)
+                turned_1 = psum_filter.tile([P, RESIDUES, P], F32)
                 near = toeplitz[:, h, 0:P]
                 far = toeplitz[:, h, P : 2 * P]
                 block_0 = [field[:, BLOCKS * r, h].rearrange("p b c -> p (b c)") for r in range(RESIDUES)]
@@ -262,22 +258,44 @@ def tile_causalwaveletfieldattentionbyte_pa_kernel(
                     )
                 return h, field_t, result
 
-            short_distances = ((1, w_pow2, 0), (2, w_pow2, 1), (3, w_three, 0), (6, w_three, 1))
-            for pair in range(HEADS // 2):
-                two_heads = (multiples_of_four(2 * pair), multiples_of_four(2 * pair + 1))
-                for distance, weights, column in short_distances:
-                    for h, field_t, result in two_heads:
-                        nc.vector.scalar_tensor_tensor(
-                            out=result[:, distance:TOKENS],
-                            in0=field_t[:, 0 : TOKENS - distance],
-                            scalar=weights[:, h, column : column + 1],
-                            in1=result[:, distance:TOKENS],
-                            op0=ALU.mult,
-                            op1=ALU.add,
-                        )
-                for h, field_t, result in two_heads:
+            def add_distance(head, distance, weights, column):
+                h, field_t, result = head
+                nc.vector.scalar_tensor_tensor(
+                    out=result[:, distance:TOKENS],
+                    in0=field_t[:, 0 : TOKENS - distance],
+                    scalar=weights[:, h, column : column + 1],
+                    in1=result[:, distance:TOKENS],
+                    op0=ALU.mult,
+                    op1=ALU.add,
+                )
+
+            first_two = ((1, w_pow2, 0), (2, w_pow2, 1))
+            last_two = ((3, w_three, 0), (6, w_three, 1))
+            unfinished = [None]
+
+            def filter_step(step):
+                before = unfinished[0]
+                head = multiples_of_four(step) if step < HEADS else None
+                for j in range(2):
+                    if before is not None:
+                        add_distance(before, *last_two[j])
+                    if head is not None:
+                        add_distance(head, *first_two[j])
+                if before is not None:
+                    h, field_t, result = before
                     for b in range(BATCH):
                         nc.sync.dma_start(
                             out=out[b, h * HEAD_DIM : (h + 1) * HEAD_DIM, :],
                             in_=result[b * HEAD_DIM : (b + 1) * HEAD_DIM, :],
                         )
+                unfinished[0] = head
+
+            for t in range(TOKEN_TILES):
+                field_of(t, 0)
+            tiles_per_head = TOKEN_TILES // heads_per_bank
+            for t in range(TOKEN_TILES):
+                field_of(t, 1)
+                if t % tiles_per_head == tiles_per_head - 1:
+                    filter_step(t // tiles_per_head)
+            for step in range(heads_per_bank, HEADS + 1):
+                filter_step(step)

@@ -25,6 +25,7 @@ BLOCKS = TOKENS // (RESIDUES * P)
 RA = RESIDUES * BLOCKS
 TOKEN_TILES = RA * BATCH
 TILES_PER_BANK = BANK // P
+SPREAD_ROWS = 20
 T0, T1, T2, T3 = 0.4829629131445341, 0.8365163037378079, 0.2241438680420134, -0.1294095225512604
 
 FLOPS = 2 * ALL_TOKENS * WIDTH * 2 * CHANNELS
@@ -36,28 +37,26 @@ def tile_causalwaveletfieldattentionbyte_pa_kernel(
     nc = tc.nc
     with ExitStack() as ctx:
         keep = ctx.enter_context(tc.tile_pool(name="keep", bufs=1))
-        stage = ctx.enter_context(tc.tile_pool(name="stage", bufs=3))
-        psum_proj = ctx.enter_context(tc.psum_pool(name="psum_proj", bufs=4))
-        psum_filter = ctx.enter_context(tc.psum_pool(name="psum_filter", bufs=1))
 
         w_planes = keep.tile([P, CHANNELS], U8, align_bytes=64)
         nc.vector.memset(w_planes[:].bitcast(I32), 0)
-        for w_index, scales in enumerate((k_w_scales, v_w_scales)):
-            for quadrant in range(4):
-                first = 32 * quadrant + 4 * PASSES * w_index
-                nc.sync.dma_start(
-                    out=w_planes[first : first + 4 * PASSES, :].bitcast(I32),
-                    in_=scales[:, 4 * quadrant : 4 * quadrant + 4, :].bitcast(I32),
-                )
 
-        gain_rows = keep.tile([P, SCALES * HEADS], BF16)
+        small_rows = keep.tile([P, P], BF16)
+        nc.vector.memset(small_rows[:], 0.0)
+        bias_rows = CHANNELS // P
+        gains_flat = scale_gain.rearrange("j h -> (j h)")
+        nc.scalar.dma_start(out=small_rows[0:bias_rows, :], in_=k_b.rearrange("(row c) -> row c", c=P))
         nc.scalar.dma_start(
-            out=gain_rows[:], in_=scale_gain.rearrange("j h -> (j h)").partition_broadcast(P)
+            out=small_rows[bias_rows : 2 * bias_rows, :], in_=v_b.rearrange("(row c) -> row c", c=P)
         )
-        k_bias = keep.tile([P, CHANNELS], BF16)
-        nc.scalar.dma_start(out=k_bias[:], in_=k_b.partition_broadcast(P))
-        v_bias = keep.tile([P, CHANNELS], BF16)
-        nc.scalar.dma_start(out=v_bias[:], in_=v_b.partition_broadcast(P))
+        nc.scalar.dma_start(
+            out=small_rows[2 * bias_rows : 2 * bias_rows + 1, :],
+            in_=gains_flat[0:P].rearrange("(row c) -> row c", row=1),
+        )
+        nc.scalar.dma_start(
+            out=small_rows[2 * bias_rows + 1 : 2 * bias_rows + 2, 0 : SCALES * HEADS - P],
+            in_=gains_flat[P : SCALES * HEADS].rearrange("(row c) -> row c", row=1),
+        )
 
         ident = keep.tile([P, P], F32)
         make_identity(nc, ident[:])
@@ -71,12 +70,20 @@ def tile_causalwaveletfieldattentionbyte_pa_kernel(
         norm2 = keep.tile([P, TOKEN_TILES, HEADS], F32)
         norm = keep.tile([P, TOKEN_TILES, HEADS], F32)
         gain_shape = [P, HEADS, SCALES]
+        spread = keep.tile([P, SPREAD_ROWS, P], F32)
+        k_bias = spread[:, 0:bias_rows, :].rearrange("p row c -> p (row c)")
+        v_bias = spread[:, bias_rows : 2 * bias_rows, :].rearrange("p row c -> p (row c)")
+        gain_rows = spread[:, 2 * bias_rows : 2 * bias_rows + 2, :].rearrange("p row c -> p (row c)")[
+            :, 0 : SCALES * HEADS
+        ]
         w_pow2 = keep.tile(gain_shape, F32)
         w_three = keep.tile(gain_shape, F32)
 
         with (
             tc.tile_pool(name="early", bufs=1) as early,
-            tc.tile_pool(name="regroup", bufs=3) as regroup,
+            tc.tile_pool(name="stage", bufs=3) as stage,
+            tc.psum_pool(name="psum_front", bufs=2) as psum_x,
+            tc.psum_pool(name="psum_proj", bufs=3) as psum,
         ):
             x_sb = early.tile([P, RA, BATCH, WIDTH], BF16)
             for r in range(RESIDUES):
@@ -86,14 +93,38 @@ def tile_causalwaveletfieldattentionbyte_pa_kernel(
                         in_=x[b].rearrange("(a i r) d -> r i a d", i=P, r=RESIDUES)[r],
                     )
                 if r == 0:
+                    for w_index, scales in enumerate((k_w_scales, v_w_scales)):
+                        for quadrant in range(4):
+                            first = 32 * quadrant + 4 * PASSES * w_index
+                            nc.sync.dma_start(
+                                out=w_planes[first : first + 4 * PASSES, :].bitcast(I32),
+                                in_=scales[:, 4 * quadrant : 4 * quadrant + 4, :].bitcast(I32),
+                            )
                     for words, packed in ((k_words, k_w_words), (v_words, v_w_words)):
                         nc.sync.dma_start(
                             out=words[:].bitcast(I32),
                             in_=packed.rearrange("g p n t -> p g (n t)").bitcast(I32),
                         )
 
+            small_rows_f32 = early.tile([P, P], F32)
+            nc.vector.tensor_copy(out=small_rows_f32[:], in_=small_rows[:])
+            small_cols_ps = psum_x.tile([P, P], F32, tag="xt")
+            nc.tensor.transpose(small_cols_ps[:], small_rows_f32[:], ident[:])
+            small_cols = early.tile([P, SPREAD_ROWS], F32)
+            nc.vector.tensor_copy(out=small_cols[:], in_=small_cols_ps[:, 0:SPREAD_ROWS])
+            for bank in range(SPREAD_ROWS // TILES_PER_BANK):
+                spread_ps = psum_x.tile([P, TILES_PER_BANK, P], F32, tag="xt")
+                for s in range(TILES_PER_BANK):
+                    row = bank * TILES_PER_BANK + s
+                    nc.tensor.transpose(
+                        spread_ps[:, s, :], small_cols[:, row : row + 1].to_broadcast([P, P]), ident[:]
+                    )
+                nc.vector.tensor_copy(
+                    out=spread[:, bank * TILES_PER_BANK : (bank + 1) * TILES_PER_BANK, :], in_=spread_ps[:]
+                )
+
             logit = early.tile(gain_shape, F32)
-            nc.vector.tensor_copy(out=logit[:], in_=gain_rows[:].rearrange("p (j h) -> p h j", h=HEADS))
+            nc.vector.tensor_copy(out=logit[:], in_=gain_rows.rearrange("p (j h) -> p h j", h=HEADS))
             top = early.tile([P, HEADS], F32)
             nc.vector.tensor_reduce(out=top[:], in_=logit[:], axis=AXIS_X, op=ALU.max)
             nc.vector.tensor_tensor(
@@ -130,7 +161,7 @@ def tile_causalwaveletfieldattentionbyte_pa_kernel(
 
             row_len = 3 * P
             weight_row = early.tile([P, HEADS, row_len], F32)
-            nc.gpsimd.memset(weight_row[:], 0.0)
+            nc.vector.memset(weight_row[:], 0.0)
             nc.vector.tensor_scalar_mul(
                 out=weight_row[:, :, P - 1 : P], in0=gain_sum[:].unsqueeze(2), scalar1=T3
             )
@@ -155,10 +186,10 @@ def tile_causalwaveletfieldattentionbyte_pa_kernel(
             tiles_per_xt = 2
             for group in range(TOKEN_TILES // TILES_PER_BANK):
                 for g in range(PASSES):
-                    grouped = regroup.tile([P, 4 * BANK], BF16, align_bytes=64)
+                    grouped = stage.tile([P, 4 * BANK], BF16, align_bytes=64)
                     grouped_words = grouped[:].bitcast(F32).rearrange("p (n u) -> p n u", u=2)
                     for half in range(TILES_PER_BANK // tiles_per_xt):
-                        xt = psum_proj.tile([P, 2, tiles_per_xt * P], F32, tag="proj")
+                        xt = psum_x.tile([P, 2, tiles_per_xt * P], F32)
                         for u in range(2):
                             for s in range(tiles_per_xt):
                                 t = group * TILES_PER_BANK + half * tiles_per_xt + s
@@ -176,61 +207,66 @@ def tile_causalwaveletfieldattentionbyte_pa_kernel(
                         out=x_codes[:, g, cols].bitcast(FP8X4), scales=x_planes[:, g, cols], in_=grouped[:]
                     )
 
-        def project(t, words, first_plane, channels):
-            acc = psum_proj.tile([P, BANK], F32, tag="proj")
-            tokens = slice(t * P, (t + 1) * P)
-            for g in range(PASSES):
-                nc.tensor.matmul_mx(
-                    out=acc[:],
-                    lhsT=x_codes[:, g, tokens].bitcast(FP8X4),
-                    lhsT_scale=x_planes[:, g, tokens],
-                    rhs=words[:, g, channels].bitcast(FP8X4),
-                    rhs_scale=w_planes[4 * (first_plane + g) : P, channels],
-                    start=(g == 0),
-                    stop=(g == PASSES - 1),
+            def project(acc, t, words, first_plane, channels):
+                tokens = slice(t * P, (t + 1) * P)
+                for g in range(PASSES):
+                    nc.tensor.matmul_mx(
+                        out=acc,
+                        lhsT=x_codes[:, g, tokens].bitcast(FP8X4),
+                        lhsT_scale=x_planes[:, g, tokens],
+                        rhs=words[:, g, channels].bitcast(FP8X4),
+                        rhs_scale=w_planes[4 * (first_plane + g) : P, channels],
+                        start=(g == 0),
+                        stop=(g == PASSES - 1),
+                    )
+
+            heads_per_bank = BANK // HEAD_DIM
+            for t in range(TOKEN_TILES):
+                ra, b = divmod(t, BATCH)
+                for half in range(CHANNELS // BANK):
+                    channels = slice(half * BANK, (half + 1) * BANK)
+                    k_ps = psum.tile([P, BANK], F32)
+                    project(k_ps[:], t, k_words, 0, channels)
+                    k_biased = stage.tile([P, BANK], F32)
+                    nc.vector.tensor_tensor(out=k_biased[:], in0=k_ps[:], in1=k_bias[:, channels], op=ALU.add)
+                    squares = stage.tile([P, BANK], F32)
+                    for e in range(heads_per_bank):
+                        h = half * heads_per_bank + e
+                        nc.scalar.activation(
+                            out=squares[:, e * HEAD_DIM : (e + 1) * HEAD_DIM],
+                            in_=k_biased[:, e * HEAD_DIM : (e + 1) * HEAD_DIM],
+                            func=ACT.Square,
+                            accum_out=norm2[:, t, h : h + 1],
+                        )
+                for half in range(CHANNELS // BANK):
+                    channels = slice(half * BANK, (half + 1) * BANK)
+                    heads = slice(half * heads_per_bank, (half + 1) * heads_per_bank)
+                    v_ps = psum.tile([P, BANK], F32)
+                    project(v_ps[:], t, v_words, PASSES, channels)
+                    nc.vector.tensor_tensor(
+                        out=field[:, ra, heads, b, :],
+                        in0=v_ps[:].rearrange("p (h c) -> p h c", c=HEAD_DIM),
+                        in1=v_bias[:, channels].rearrange("p (h c) -> p h c", c=HEAD_DIM),
+                        op=ALU.add,
+                    )
+                nc.scalar.activation(out=norm[:, t, :], in_=norm2[:, t, :], func=ACT.Sqrt)
+                nc.gpsimd.tensor_tensor(
+                    out=field[:, ra, :, b, :],
+                    in0=field[:, ra, :, b, :],
+                    in1=norm[:, t, :].unsqueeze(2).to_broadcast([P, HEADS, HEAD_DIM]),
+                    op=ALU.mult,
                 )
-            return acc
 
-        heads_per_bank = BANK // HEAD_DIM
-
-        def field_of(t, half):
-            ra, b = divmod(t, BATCH)
-            channels = slice(half * BANK, (half + 1) * BANK)
-            heads = slice(half * heads_per_bank, (half + 1) * heads_per_bank)
-            k_ps = project(t, k_words, 0, channels)
-            k_biased = stage.tile([P, BANK], F32)
-            nc.vector.tensor_tensor(out=k_biased[:], in0=k_ps[:], in1=k_bias[:, channels], op=ALU.add)
-            squares = stage.tile([P, BANK], F32)
-            for e in range(heads_per_bank):
-                h = half * heads_per_bank + e
-                nc.scalar.activation(
-                    out=squares[:, e * HEAD_DIM : (e + 1) * HEAD_DIM],
-                    in_=k_biased[:, e * HEAD_DIM : (e + 1) * HEAD_DIM],
-                    func=ACT.Square,
-                    accum_out=norm2[:, t, h : h + 1],
-                )
-            nc.scalar.activation(out=norm[:, t, heads], in_=norm2[:, t, heads], func=ACT.Sqrt)
-            v_ps = project(t, v_words, PASSES, channels)
-            nc.vector.tensor_tensor(
-                out=field[:, ra, heads, b, :],
-                in0=v_ps[:].rearrange("p (h c) -> p h c", c=HEAD_DIM),
-                in1=v_bias[:, channels].rearrange("p (h c) -> p h c", c=HEAD_DIM),
-                op=ALU.add,
-            )
-            nc.gpsimd.tensor_tensor(
-                out=field[:, ra, heads, b, :],
-                in0=field[:, ra, heads, b, :],
-                in1=norm[:, t, heads].unsqueeze(2).to_broadcast([P, heads_per_bank, HEAD_DIM]),
-                op=ALU.mult,
-            )
-
-        with tc.tile_pool(name="late", bufs=4) as late:
+        with (
+            tc.tile_pool(name="late", bufs=4) as late,
+            tc.psum_pool(name="psum_filter", bufs=2) as psum,
+        ):
 
             def multiples_of_four(h):
-                sums_0 = psum_filter.tile([P, RESIDUES, P], F32)
-                sums_1 = psum_filter.tile([P, RESIDUES, P], F32)
-                turned_0 = psum_filter.tile([P, RESIDUES, P], F32)
-                turned_1 = psum_filter.tile([P, RESIDUES, P], F32)
+                sums_0 = psum.tile([P, RESIDUES, P], F32)
+                sums_1 = psum.tile([P, RESIDUES, P], F32)
+                turned_0 = psum.tile([P, RESIDUES, P], F32)
+                turned_1 = psum.tile([P, RESIDUES, P], F32)
                 near = toeplitz[:, h, 0:P]
                 far = toeplitz[:, h, P : 2 * P]
                 block_0 = [field[:, BLOCKS * r, h].rearrange("p b c -> p (b c)") for r in range(RESIDUES)]
@@ -258,44 +294,22 @@ def tile_causalwaveletfieldattentionbyte_pa_kernel(
                     )
                 return h, field_t, result
 
-            def add_distance(head, distance, weights, column):
-                h, field_t, result = head
-                nc.vector.scalar_tensor_tensor(
-                    out=result[:, distance:TOKENS],
-                    in0=field_t[:, 0 : TOKENS - distance],
-                    scalar=weights[:, h, column : column + 1],
-                    in1=result[:, distance:TOKENS],
-                    op0=ALU.mult,
-                    op1=ALU.add,
-                )
-
-            first_two = ((1, w_pow2, 0), (2, w_pow2, 1))
-            last_two = ((3, w_three, 0), (6, w_three, 1))
-            unfinished = [None]
-
-            def filter_step(step):
-                before = unfinished[0]
-                head = multiples_of_four(step) if step < HEADS else None
-                for j in range(2):
-                    if before is not None:
-                        add_distance(before, *last_two[j])
-                    if head is not None:
-                        add_distance(head, *first_two[j])
-                if before is not None:
-                    h, field_t, result = before
+            short_distances = ((1, w_pow2, 0), (2, w_pow2, 1), (3, w_three, 0), (6, w_three, 1))
+            for pair in range(HEADS // 2):
+                two_heads = (multiples_of_four(2 * pair), multiples_of_four(2 * pair + 1))
+                for distance, weights, column in short_distances:
+                    for h, field_t, result in two_heads:
+                        nc.vector.scalar_tensor_tensor(
+                            out=result[:, distance:TOKENS],
+                            in0=field_t[:, 0 : TOKENS - distance],
+                            scalar=weights[:, h, column : column + 1],
+                            in1=result[:, distance:TOKENS],
+                            op0=ALU.mult,
+                            op1=ALU.add,
+                        )
+                for h, field_t, result in two_heads:
                     for b in range(BATCH):
                         nc.sync.dma_start(
                             out=out[b, h * HEAD_DIM : (h + 1) * HEAD_DIM, :],
                             in_=result[b * HEAD_DIM : (b + 1) * HEAD_DIM, :],
                         )
-                unfinished[0] = head
-
-            for t in range(TOKEN_TILES):
-                field_of(t, 0)
-            tiles_per_head = TOKEN_TILES // heads_per_bank
-            for t in range(TOKEN_TILES):
-                field_of(t, 1)
-                if t % tiles_per_head == tiles_per_head - 1:
-                    filter_step(t // tiles_per_head)
-            for step in range(heads_per_bank, HEADS + 1):
-                filter_step(step)

@@ -25,6 +25,7 @@ BLOCKS = TOKENS // (RESIDUES * P)
 RA = RESIDUES * BLOCKS
 TOKEN_TILES = RA * BATCH
 TILES_PER_BANK = BANK // P
+PAD = 8
 SPREAD_ROWS = 20
 T0, T1, T2, T3 = 0.4829629131445341, 0.8365163037378079, 0.2241438680420134, -0.1294095225512604
 
@@ -280,36 +281,45 @@ def tile_causalwaveletfieldattentionbyte_pa_kernel(
                     nc.tensor.transpose(turned_0[:, r, :], block_0[r], ident[:])
                 for r in range(RESIDUES):
                     nc.tensor.transpose(turned_1[:, r, :], block_1[r], ident[:])
-                result = late.tile([P, TOKENS], F32)
-                field_t = late.tile([P, TOKENS], F32)
-                for bank, natural, a in (
-                    (sums_0, result, 0),
-                    (sums_1, result, 1),
-                    (turned_0, field_t, 0),
-                    (turned_1, field_t, 1),
-                ):
+                result = late.tile([P, TOKENS + PAD], F32)
+                nc.gpsimd.memset(result[:, TOKENS : TOKENS + PAD], 0.0)
+                for a, bank in enumerate((sums_0, sums_1)):
                     nc.scalar.copy(
-                        out=natural[:, a * BANK : (a + 1) * BANK].rearrange("p (i r) -> p i r", r=RESIDUES),
+                        out=result[:, a * BANK : (a + 1) * BANK].rearrange("p (i r) -> p i r", r=RESIDUES),
                         in_=bank[:].rearrange("p r i -> p i r"),
                     )
-                return h, field_t, result
+                sixth = late.tile([P, TOKENS], F32)
+                for a, bank in enumerate((turned_0, turned_1)):
+                    nc.scalar.activation(
+                        out=sixth[:, a * BANK : (a + 1) * BANK].rearrange("p (i r) -> p i r", r=RESIDUES),
+                        in_=bank[:].rearrange("p r i -> p i r"),
+                        func=ACT.Copy,
+                        scale=w_three[:, h, 1:2],
+                    )
+                return h, (turned_0, turned_1), result, sixth
 
-            short_distances = ((1, w_pow2, 0), (2, w_pow2, 1), (3, w_three, 0), (6, w_three, 1))
+            short_distances = ((1, w_pow2, 0), (2, w_pow2, 1), (3, w_three, 0))
             for pair in range(HEADS // 2):
                 two_heads = (multiples_of_four(2 * pair), multiples_of_four(2 * pair + 1))
-                for distance, weights, column in short_distances:
-                    for h, field_t, result in two_heads:
-                        nc.vector.scalar_tensor_tensor(
-                            out=result[:, distance:TOKENS],
-                            in0=field_t[:, 0 : TOKENS - distance],
-                            scalar=weights[:, h, column : column + 1],
-                            in1=result[:, distance:TOKENS],
-                            op0=ALU.mult,
-                            op1=ALU.add,
-                        )
-                for h, field_t, result in two_heads:
+                for a in range(BLOCKS):
+                    for distance, weights, column in short_distances:
+                        for h, turned, result, sixth in two_heads:
+                            first = a * BANK + distance
+                            target = result[:, first : first + BANK].rearrange("p (i r) -> p i r", r=RESIDUES)
+                            nc.vector.scalar_tensor_tensor(
+                                out=target,
+                                in0=turned[a][:].rearrange("p r i -> p i r"),
+                                scalar=weights[:, h, column : column + 1],
+                                in1=target,
+                                op0=ALU.mult,
+                                op1=ALU.add,
+                            )
+                for h, turned, result, sixth in two_heads:
+                    nc.gpsimd.tensor_tensor(
+                        out=result[:, 6:TOKENS], in0=result[:, 6:TOKENS], in1=sixth[:, 0 : TOKENS - 6], op=ALU.add
+                    )
                     for b in range(BATCH):
                         nc.sync.dma_start(
                             out=out[b, h * HEAD_DIM : (h + 1) * HEAD_DIM, :],
-                            in_=result[b * HEAD_DIM : (b + 1) * HEAD_DIM, :],
+                            in_=result[b * HEAD_DIM : (b + 1) * HEAD_DIM, 0:TOKENS],
                         )

@@ -120,7 +120,7 @@ def tile_causalwaveletfieldattentionbyte_pa_kernel(
                     nc.tensor.transpose(
                         spread_ps[:, s, :], small_cols[:, row : row + 1].to_broadcast([P, P]), ident[:]
                     )
-                nc.vector.tensor_copy(
+                nc.scalar.copy(
                     out=spread[:, bank * TILES_PER_BANK : (bank + 1) * TILES_PER_BANK, :], in_=spread_ps[:]
                 )
 
@@ -163,15 +163,15 @@ def tile_causalwaveletfieldattentionbyte_pa_kernel(
             row_len = 3 * P
             weight_row = early.tile([P, HEADS, row_len], F32)
             nc.vector.memset(weight_row[:], 0.0)
-            nc.vector.tensor_scalar_mul(
+            nc.gpsimd.tensor_scalar_mul(
                 out=weight_row[:, :, P - 1 : P], in0=gain_sum[:].unsqueeze(2), scalar1=T3
             )
             for i in range(2, SCALES):
                 at = P - 1 + 2 ** (i - 2)
-                nc.vector.tensor_copy(out=weight_row[:, :, at : at + 1], in_=w_pow2[:, :, i : i + 1])
+                nc.gpsimd.tensor_copy(out=weight_row[:, :, at : at + 1], in_=w_pow2[:, :, i : i + 1])
             for j in range(2, SCALES - 1):
                 at = P - 1 + 3 * 2 ** (j - 2)
-                nc.vector.tensor_copy(out=weight_row[:, :, at : at + 1], in_=w_three[:, :, j : j + 1])
+                nc.gpsimd.tensor_copy(out=weight_row[:, :, at : at + 1], in_=w_three[:, :, j : j + 1])
             flat_out = out.rearrange("b c n -> (b c n)")
             pitch = HEADS * row_len
             nc.sync.dma_start(
@@ -260,66 +260,83 @@ def tile_causalwaveletfieldattentionbyte_pa_kernel(
 
         with (
             tc.tile_pool(name="late", bufs=4) as late,
-            tc.psum_pool(name="psum_filter", bufs=2) as psum,
+            tc.psum_pool(name="psum_sums", bufs=3) as psum_sums,
+            tc.psum_pool(name="psum_turned", bufs=5) as psum_turned,
         ):
+            short_distances = ((1, w_pow2, 0), (2, w_pow2, 1), (3, w_three, 0))
+            natural = "p (i r) -> p i r"
+            permuted = "p r i -> p i r"
+            tiles_of_head = {}
+            turned_of_unit = {}
 
-            def multiples_of_four(h):
-                sums_0 = psum.tile([P, RESIDUES, P], F32)
-                sums_1 = psum.tile([P, RESIDUES, P], F32)
-                turned_0 = psum.tile([P, RESIDUES, P], F32)
-                turned_1 = psum.tile([P, RESIDUES, P], F32)
+            def multiples_of_four(h, a):
+                if a == 0:
+                    result = late.tile([P, BLOCKS, BANK + PAD], F32)
+                    nc.gpsimd.memset(result[:, :, BANK : BANK + PAD], 0.0)
+                    sixth = late.tile([P, TOKENS], F32)
+                    tiles_of_head[h] = (result, sixth)
+                result, sixth = tiles_of_head[h]
                 near = toeplitz[:, h, 0:P]
                 far = toeplitz[:, h, P : 2 * P]
                 block_0 = [field[:, BLOCKS * r, h].rearrange("p b c -> p (b c)") for r in range(RESIDUES)]
                 block_1 = [field[:, BLOCKS * r + 1, h].rearrange("p b c -> p (b c)") for r in range(RESIDUES)]
+                sums = psum_sums.tile([P, RESIDUES, P], F32)
                 for r in range(RESIDUES):
-                    nc.tensor.matmul(out=sums_0[:, r, :], lhsT=block_0[r], rhs=near, start=True, stop=True)
+                    if a == 0:
+                        nc.tensor.matmul(out=sums[:, r, :], lhsT=block_0[r], rhs=near, start=True, stop=True)
+                    else:
+                        nc.tensor.matmul(out=sums[:, r, :], lhsT=block_0[r], rhs=far, start=True, stop=False)
+                        nc.tensor.matmul(out=sums[:, r, :], lhsT=block_1[r], rhs=near, start=False, stop=True)
+                turned = psum_turned.tile([P, RESIDUES, P], F32)
                 for r in range(RESIDUES):
-                    nc.tensor.matmul(out=sums_1[:, r, :], lhsT=block_0[r], rhs=far, start=True, stop=False)
-                    nc.tensor.matmul(out=sums_1[:, r, :], lhsT=block_1[r], rhs=near, start=False, stop=True)
-                for r in range(RESIDUES):
-                    nc.tensor.transpose(turned_0[:, r, :], block_0[r], ident[:])
-                for r in range(RESIDUES):
-                    nc.tensor.transpose(turned_1[:, r, :], block_1[r], ident[:])
-                result = late.tile([P, TOKENS + PAD], F32)
-                nc.gpsimd.memset(result[:, TOKENS : TOKENS + PAD], 0.0)
-                for a, bank in enumerate((sums_0, sums_1)):
-                    nc.scalar.copy(
-                        out=result[:, a * BANK : (a + 1) * BANK].rearrange("p (i r) -> p i r", r=RESIDUES),
-                        in_=bank[:].rearrange("p r i -> p i r"),
-                    )
-                sixth = late.tile([P, TOKENS], F32)
-                for a, bank in enumerate((turned_0, turned_1)):
-                    nc.scalar.activation(
-                        out=sixth[:, a * BANK : (a + 1) * BANK].rearrange("p (i r) -> p i r", r=RESIDUES),
-                        in_=bank[:].rearrange("p r i -> p i r"),
-                        func=ACT.Copy,
-                        scale=w_three[:, h, 1:2],
-                    )
-                return h, (turned_0, turned_1), result, sixth
+                    nc.tensor.transpose(turned[:, r, :], (block_0, block_1)[a][r], ident[:])
+                turned_of_unit[(h, a)] = turned
+                nc.scalar.copy(out=result[:, a, 0:BANK].rearrange(natural, r=RESIDUES), in_=sums[:].rearrange(permuted))
+                nc.scalar.activation(
+                    out=sixth[:, a * BANK : (a + 1) * BANK].rearrange(natural, r=RESIDUES),
+                    in_=turned[:].rearrange(permuted),
+                    func=ACT.Copy,
+                    scale=w_three[:, h, 1:2],
+                )
 
-            short_distances = ((1, w_pow2, 0), (2, w_pow2, 1), (3, w_three, 0))
-            for pair in range(HEADS // 2):
-                two_heads = (multiples_of_four(2 * pair), multiples_of_four(2 * pair + 1))
-                for a in range(BLOCKS):
-                    for distance, weights, column in short_distances:
-                        for h, turned, result, sixth in two_heads:
-                            first = a * BANK + distance
-                            target = result[:, first : first + BANK].rearrange("p (i r) -> p i r", r=RESIDUES)
-                            nc.vector.scalar_tensor_tensor(
-                                out=target,
-                                in0=turned[a][:].rearrange("p r i -> p i r"),
-                                scalar=weights[:, h, column : column + 1],
-                                in1=target,
-                                op0=ALU.mult,
-                                op1=ALU.add,
-                            )
-                for h, turned, result, sixth in two_heads:
+            def short_distance(h, a, which):
+                distance, weights, column = short_distances[which]
+                target = tiles_of_head[h][0][:, a, distance : distance + BANK].rearrange(natural, r=RESIDUES)
+                nc.vector.scalar_tensor_tensor(
+                    out=target,
+                    in0=turned_of_unit[(h, a)][:].rearrange(permuted),
+                    scalar=weights[:, h, column : column + 1],
+                    in1=target,
+                    op0=ALU.mult,
+                    op1=ALU.add,
+                )
+
+            def finish(h, a):
+                result, sixth = tiles_of_head[h]
+                if a == 0:
                     nc.gpsimd.tensor_tensor(
-                        out=result[:, 6:TOKENS], in0=result[:, 6:TOKENS], in1=sixth[:, 0 : TOKENS - 6], op=ALU.add
+                        out=result[:, 0, 6:BANK], in0=result[:, 0, 6:BANK], in1=sixth[:, 0 : BANK - 6], op=ALU.add
                     )
-                    for b in range(BATCH):
-                        nc.sync.dma_start(
-                            out=out[b, h * HEAD_DIM : (h + 1) * HEAD_DIM, :],
-                            in_=result[b * HEAD_DIM : (b + 1) * HEAD_DIM, 0:TOKENS],
-                        )
+                else:
+                    nc.gpsimd.tensor_tensor(
+                        out=result[:, 1, 0:BANK], in0=result[:, 1, 0:BANK], in1=sixth[:, BANK - 6 : TOKENS - 6], op=ALU.add
+                    )
+                    nc.gpsimd.tensor_tensor(
+                        out=result[:, 1, 0:3], in0=result[:, 1, 0:3], in1=result[:, 0, BANK : BANK + 3], op=ALU.add
+                    )
+                for b in range(BATCH):
+                    nc.sync.dma_start(
+                        out=out[b, h * HEAD_DIM : (h + 1) * HEAD_DIM, a * BANK : (a + 1) * BANK],
+                        in_=result[b * HEAD_DIM : (b + 1) * HEAD_DIM, a, 0:BANK],
+                    )
+
+            units = [(h, a) for h in range(HEADS) for a in range(BLOCKS)]
+            for k in range(len(units) + 1):
+                if k < len(units):
+                    multiples_of_four(*units[k])
+                    short_distance(*units[k], 0)
+                if k > 0:
+                    short_distance(*units[k - 1], 2)
+                    finish(*units[k - 1])
+                if k < len(units):
+                    short_distance(*units[k], 1)

@@ -80,12 +80,22 @@ def tile_causalwaveletfieldattentionbyte_pa_kernel(
         w_pow2 = keep.tile(gain_shape, F32)
         w_three = keep.tile(gain_shape, F32)
 
+        stage = ctx.enter_context(tc.tile_pool(name="stage", bufs=3))
+        psum_acc = ctx.enter_context(tc.psum_pool(name="psum_acc", bufs=3))
+        psum_flip = ctx.enter_context(tc.psum_pool(name="psum_flip", bufs=5))
+
         with (
             tc.tile_pool(name="early", bufs=1) as early,
-            tc.tile_pool(name="stage", bufs=3) as stage,
-            tc.psum_pool(name="psum_front", bufs=2) as psum_x,
-            tc.psum_pool(name="psum_proj", bufs=3) as psum,
+            tc.tile_pool(name="stage_x", bufs=3) as stage_x,
         ):
+            def load_words(half):
+                channels = slice(half * BANK, (half + 1) * BANK)
+                for words, packed in ((k_words, k_w_words), (v_words, v_w_words)):
+                    nc.sync.dma_start(
+                        out=words[:, :, channels].bitcast(I32),
+                        in_=packed.rearrange("g p n t -> p g (n t)").bitcast(I32)[:, :, channels],
+                    )
+
             x_sb = early.tile([P, RA, BATCH, WIDTH], BF16)
             for r in range(RESIDUES):
                 for b in range(BATCH):
@@ -101,20 +111,17 @@ def tile_causalwaveletfieldattentionbyte_pa_kernel(
                                 out=w_planes[first : first + 4 * PASSES, :].bitcast(I32),
                                 in_=scales[:, 4 * quadrant : 4 * quadrant + 4, :].bitcast(I32),
                             )
-                    for words, packed in ((k_words, k_w_words), (v_words, v_w_words)):
-                        nc.sync.dma_start(
-                            out=words[:].bitcast(I32),
-                            in_=packed.rearrange("g p n t -> p g (n t)").bitcast(I32),
-                        )
+                    load_words(0)
+            load_words(1)
 
             small_rows_f32 = early.tile([P, P], F32)
             nc.vector.tensor_copy(out=small_rows_f32[:], in_=small_rows[:])
-            small_cols_ps = psum_x.tile([P, P], F32, tag="xt")
+            small_cols_ps = psum_flip.tile([P, P], F32, tag="flip")
             nc.tensor.transpose(small_cols_ps[:], small_rows_f32[:], ident[:])
             small_cols = early.tile([P, SPREAD_ROWS], F32)
             nc.vector.tensor_copy(out=small_cols[:], in_=small_cols_ps[:, 0:SPREAD_ROWS])
             for bank in range(SPREAD_ROWS // TILES_PER_BANK):
-                spread_ps = psum_x.tile([P, TILES_PER_BANK, P], F32, tag="xt")
+                spread_ps = psum_flip.tile([P, TILES_PER_BANK, P], F32, tag="flip")
                 for s in range(TILES_PER_BANK):
                     row = bank * TILES_PER_BANK + s
                     nc.tensor.transpose(
@@ -187,10 +194,10 @@ def tile_causalwaveletfieldattentionbyte_pa_kernel(
             tiles_per_xt = 2
             for group in range(TOKEN_TILES // TILES_PER_BANK):
                 for g in range(PASSES):
-                    grouped = stage.tile([P, 4 * BANK], BF16, align_bytes=64)
+                    grouped = stage_x.tile([P, 4 * BANK], BF16, align_bytes=64)
                     grouped_words = grouped[:].bitcast(F32).rearrange("p (n u) -> p n u", u=2)
                     for half in range(TILES_PER_BANK // tiles_per_xt):
-                        xt = psum_x.tile([P, 2, tiles_per_xt * P], F32)
+                        xt = psum_flip.tile([P, 2, tiles_per_xt * P], F32, tag="flip")
                         for u in range(2):
                             for s in range(tiles_per_xt):
                                 t = group * TILES_PER_BANK + half * tiles_per_xt + s
@@ -208,62 +215,61 @@ def tile_causalwaveletfieldattentionbyte_pa_kernel(
                         out=x_codes[:, g, cols].bitcast(FP8X4), scales=x_planes[:, g, cols], in_=grouped[:]
                     )
 
-            def project(acc, t, words, first_plane, channels):
-                tokens = slice(t * P, (t + 1) * P)
-                for g in range(PASSES):
-                    nc.tensor.matmul_mx(
-                        out=acc,
-                        lhsT=x_codes[:, g, tokens].bitcast(FP8X4),
-                        lhsT_scale=x_planes[:, g, tokens],
-                        rhs=words[:, g, channels].bitcast(FP8X4),
-                        rhs_scale=w_planes[4 * (first_plane + g) : P, channels],
-                        start=(g == 0),
-                        stop=(g == PASSES - 1),
-                    )
+        def project(acc, t, words, first_plane, channels):
+            tokens = slice(t * P, (t + 1) * P)
+            for g in range(PASSES):
+                nc.tensor.matmul_mx(
+                    out=acc,
+                    lhsT=x_codes[:, g, tokens].bitcast(FP8X4),
+                    lhsT_scale=x_planes[:, g, tokens],
+                    rhs=words[:, g, channels].bitcast(FP8X4),
+                    rhs_scale=w_planes[4 * (first_plane + g) : P, channels],
+                    start=(g == 0),
+                    stop=(g == PASSES - 1),
+                )
 
-            heads_per_bank = BANK // HEAD_DIM
-            for t in range(TOKEN_TILES):
+        heads_per_bank = BANK // HEAD_DIM
+
+        def project_step(half, t):
+            if True:
+                channels = slice(half * BANK, (half + 1) * BANK)
+                heads = slice(half * heads_per_bank, (half + 1) * heads_per_bank)
                 ra, b = divmod(t, BATCH)
-                for half in range(CHANNELS // BANK):
-                    channels = slice(half * BANK, (half + 1) * BANK)
-                    k_ps = psum.tile([P, BANK], F32)
-                    project(k_ps[:], t, k_words, 0, channels)
-                    k_biased = stage.tile([P, BANK], F32)
-                    nc.vector.tensor_tensor(out=k_biased[:], in0=k_ps[:], in1=k_bias[:, channels], op=ALU.add)
-                    squares = stage.tile([P, BANK], F32)
-                    for e in range(heads_per_bank):
-                        h = half * heads_per_bank + e
-                        nc.scalar.activation(
-                            out=squares[:, e * HEAD_DIM : (e + 1) * HEAD_DIM],
-                            in_=k_biased[:, e * HEAD_DIM : (e + 1) * HEAD_DIM],
-                            func=ACT.Square,
-                            accum_out=norm2[:, t, h : h + 1],
-                        )
-                for half in range(CHANNELS // BANK):
-                    channels = slice(half * BANK, (half + 1) * BANK)
-                    heads = slice(half * heads_per_bank, (half + 1) * heads_per_bank)
-                    v_ps = psum.tile([P, BANK], F32)
-                    project(v_ps[:], t, v_words, PASSES, channels)
-                    nc.vector.tensor_tensor(
-                        out=field[:, ra, heads, b, :],
-                        in0=v_ps[:].rearrange("p (h c) -> p h c", c=HEAD_DIM),
-                        in1=v_bias[:, channels].rearrange("p (h c) -> p h c", c=HEAD_DIM),
-                        op=ALU.add,
+                k_ps = psum_acc.tile([P, BANK], F32, tag="acc")
+                project(k_ps[:], t, k_words, 0, channels)
+                k_biased = stage.tile([P, BANK], F32)
+                nc.vector.tensor_tensor(out=k_biased[:], in0=k_ps[:], in1=k_bias[:, channels], op=ALU.add)
+                squares = stage.tile([P, BANK], F32)
+                for e in range(heads_per_bank):
+                    h = half * heads_per_bank + e
+                    nc.scalar.activation(
+                        out=squares[:, e * HEAD_DIM : (e + 1) * HEAD_DIM],
+                        in_=k_biased[:, e * HEAD_DIM : (e + 1) * HEAD_DIM],
+                        func=ACT.Square,
+                        accum_out=norm2[:, t, h : h + 1],
                     )
-                nc.scalar.activation(out=norm[:, t, :], in_=norm2[:, t, :], func=ACT.Sqrt)
+                v_ps = psum_acc.tile([P, BANK], F32, tag="acc")
+                project(v_ps[:], t, v_words, PASSES, channels)
+                nc.vector.tensor_tensor(
+                    out=field[:, ra, heads, b, :],
+                    in0=v_ps[:].rearrange("p (h c) -> p h c", c=HEAD_DIM),
+                    in1=v_bias[:, channels].rearrange("p (h c) -> p h c", c=HEAD_DIM),
+                    op=ALU.add,
+                )
+                nc.scalar.activation(out=norm[:, t, heads], in_=norm2[:, t, heads], func=ACT.Sqrt)
                 nc.gpsimd.tensor_tensor(
-                    out=field[:, ra, :, b, :],
-                    in0=field[:, ra, :, b, :],
-                    in1=norm[:, t, :].unsqueeze(2).to_broadcast([P, HEADS, HEAD_DIM]),
+                    out=field[:, ra, heads, b, :],
+                    in0=field[:, ra, heads, b, :],
+                    in1=norm[:, t, heads].unsqueeze(2).to_broadcast([P, heads_per_bank, HEAD_DIM]),
                     op=ALU.mult,
                 )
 
-        with (
-            tc.tile_pool(name="late", bufs=4) as late,
-            tc.psum_pool(name="psum_sums", bufs=3) as psum_sums,
-            tc.psum_pool(name="psum_turned", bufs=5) as psum_turned,
-        ):
-            short_distances = ((1, w_pow2, 0), (2, w_pow2, 1), (3, w_three, 0))
+        for t in range(TOKEN_TILES):
+            project_step(0, t)
+
+        with tc.tile_pool(name="late", bufs=4) as late:
+            short_distances = ((1, w_pow2, 0), (2, w_pow2, 1), (3, w_three, 0), (6, w_three, 1))
+            last_head = HEADS - 1
             natural = "p (i r) -> p i r"
             permuted = "p r i -> p i r"
             tiles_of_head = {}
@@ -280,24 +286,25 @@ def tile_causalwaveletfieldattentionbyte_pa_kernel(
                 far = toeplitz[:, h, P : 2 * P]
                 block_0 = [field[:, BLOCKS * r, h].rearrange("p b c -> p (b c)") for r in range(RESIDUES)]
                 block_1 = [field[:, BLOCKS * r + 1, h].rearrange("p b c -> p (b c)") for r in range(RESIDUES)]
-                sums = psum_sums.tile([P, RESIDUES, P], F32)
+                sums = psum_acc.tile([P, RESIDUES, P], F32, tag="acc")
                 for r in range(RESIDUES):
                     if a == 0:
                         nc.tensor.matmul(out=sums[:, r, :], lhsT=block_0[r], rhs=near, start=True, stop=True)
                     else:
                         nc.tensor.matmul(out=sums[:, r, :], lhsT=block_0[r], rhs=far, start=True, stop=False)
                         nc.tensor.matmul(out=sums[:, r, :], lhsT=block_1[r], rhs=near, start=False, stop=True)
-                turned = psum_turned.tile([P, RESIDUES, P], F32)
+                turned = psum_flip.tile([P, RESIDUES, P], F32, tag="flip")
                 for r in range(RESIDUES):
                     nc.tensor.transpose(turned[:, r, :], (block_0, block_1)[a][r], ident[:])
                 turned_of_unit[(h, a)] = turned
                 nc.scalar.copy(out=result[:, a, 0:BANK].rearrange(natural, r=RESIDUES), in_=sums[:].rearrange(permuted))
-                nc.scalar.activation(
-                    out=sixth[:, a * BANK : (a + 1) * BANK].rearrange(natural, r=RESIDUES),
-                    in_=turned[:].rearrange(permuted),
-                    func=ACT.Copy,
-                    scale=w_three[:, h, 1:2],
-                )
+                if h != last_head:
+                    nc.scalar.activation(
+                        out=sixth[:, a * BANK : (a + 1) * BANK].rearrange(natural, r=RESIDUES),
+                        in_=turned[:].rearrange(permuted),
+                        func=ACT.Copy,
+                        scale=w_three[:, h, 1:2],
+                    )
 
             def short_distance(h, a, which):
                 distance, weights, column = short_distances[which]
@@ -313,7 +320,9 @@ def tile_causalwaveletfieldattentionbyte_pa_kernel(
 
             def finish(h, a):
                 result, sixth = tiles_of_head[h]
-                if a == 0:
+                if h == last_head:
+                    short_distance(h, a, 3)
+                elif a == 0:
                     nc.gpsimd.tensor_tensor(
                         out=result[:, 0, 6:BANK], in0=result[:, 0, 6:BANK], in1=sixth[:, 0 : BANK - 6], op=ALU.add
                     )
@@ -321,8 +330,10 @@ def tile_causalwaveletfieldattentionbyte_pa_kernel(
                     nc.gpsimd.tensor_tensor(
                         out=result[:, 1, 0:BANK], in0=result[:, 1, 0:BANK], in1=sixth[:, BANK - 6 : TOKENS - 6], op=ALU.add
                     )
-                    nc.gpsimd.tensor_tensor(
-                        out=result[:, 1, 0:3], in0=result[:, 1, 0:3], in1=result[:, 0, BANK : BANK + 3], op=ALU.add
+                if a == 1:
+                    carrier = nc.vector if h == last_head else nc.gpsimd
+                    carrier.tensor_tensor(
+                        out=result[:, 1, 0:PAD], in0=result[:, 1, 0:PAD], in1=result[:, 0, BANK : BANK + PAD], op=ALU.add
                     )
                 for b in range(BATCH):
                     nc.sync.dma_start(
@@ -331,7 +342,8 @@ def tile_causalwaveletfieldattentionbyte_pa_kernel(
                     )
 
             units = [(h, a) for h in range(HEADS) for a in range(BLOCKS)]
-            for k in range(len(units) + 1):
+
+            def filter_step(k):
                 if k < len(units):
                     multiples_of_four(*units[k])
                     short_distance(*units[k], 0)
@@ -340,3 +352,9 @@ def tile_causalwaveletfieldattentionbyte_pa_kernel(
                     finish(*units[k - 1])
                 if k < len(units):
                     short_distance(*units[k], 1)
+
+            for t in range(TOKEN_TILES):
+                project_step(1, t)
+                filter_step(t)
+            for k in range(TOKEN_TILES, len(units) + 1):
+                filter_step(k)

@@ -80,7 +80,7 @@ def tile_causalwaveletfieldattentionbyte_pa_kernel(
         w_pow2 = keep.tile(gain_shape, F32)
         w_three = keep.tile(gain_shape, F32)
 
-        stage = ctx.enter_context(tc.tile_pool(name="stage", bufs=3))
+        stage = ctx.enter_context(tc.tile_pool(name="stage", bufs=4))
         psum_acc = ctx.enter_context(tc.psum_pool(name="psum_acc", bufs=3))
         psum_flip = ctx.enter_context(tc.psum_pool(name="psum_flip", bufs=5))
 
@@ -267,21 +267,27 @@ def tile_causalwaveletfieldattentionbyte_pa_kernel(
         for t in range(TOKEN_TILES):
             project_step(0, t)
 
-        with tc.tile_pool(name="late", bufs=4) as late:
+        with tc.tile_pool(name="late", bufs=6) as late:
             short_distances = ((1, w_pow2, 0), (2, w_pow2, 1), (3, w_three, 0), (6, w_three, 1))
-            last_head = HEADS - 1
             natural = "p (i r) -> p i r"
             permuted = "p r i -> p i r"
-            tiles_of_head = {}
+            units = [(h, a) for h in range(HEADS) for a in range(BLOCKS)]
+            result_of_head = {}
             turned_of_unit = {}
+            products_of_unit = {}
 
-            def multiples_of_four(h, a):
+            def handed_over(k):
+                if units[k][0] == HEADS - 1:
+                    return ()
+                return (3,)
+
+            def multiples_of_four(k):
+                h, a = units[k]
                 if a == 0:
                     result = late.tile([P, BLOCKS, BANK + PAD], F32)
                     nc.gpsimd.memset(result[:, :, BANK : BANK + PAD], 0.0)
-                    sixth = late.tile([P, TOKENS], F32)
-                    tiles_of_head[h] = (result, sixth)
-                result, sixth = tiles_of_head[h]
+                    result_of_head[h] = result
+                result = result_of_head[h]
                 near = toeplitz[:, h, 0:P]
                 far = toeplitz[:, h, P : 2 * P]
                 block_0 = [field[:, BLOCKS * r, h].rearrange("p b c -> p (b c)") for r in range(RESIDUES)]
@@ -296,42 +302,41 @@ def tile_causalwaveletfieldattentionbyte_pa_kernel(
                 turned = psum_flip.tile([P, RESIDUES, P], F32, tag="flip")
                 for r in range(RESIDUES):
                     nc.tensor.transpose(turned[:, r, :], (block_0, block_1)[a][r], ident[:])
-                turned_of_unit[(h, a)] = turned
+                turned_of_unit[k] = turned
                 nc.scalar.copy(out=result[:, a, 0:BANK].rearrange(natural, r=RESIDUES), in_=sums[:].rearrange(permuted))
-                if h != last_head:
+                products_of_unit[k] = []
+                for place, which in enumerate(handed_over(k)):
+                    distance, weights, column = short_distances[which]
+                    product = late.tile([P, BANK], F32, tag="product%d" % place)
                     nc.scalar.activation(
-                        out=sixth[:, a * BANK : (a + 1) * BANK].rearrange(natural, r=RESIDUES),
+                        out=product[:].rearrange(natural, r=RESIDUES),
                         in_=turned[:].rearrange(permuted),
                         func=ACT.Copy,
-                        scale=w_three[:, h, 1:2],
+                        scale=weights[:, h, column : column + 1],
                     )
+                    products_of_unit[k].append((distance, product))
 
-            def short_distance(h, a, which):
+            def short_distance(k, which):
+                h, a = units[k]
                 distance, weights, column = short_distances[which]
-                target = tiles_of_head[h][0][:, a, distance : distance + BANK].rearrange(natural, r=RESIDUES)
+                target = result_of_head[h][:, a, distance : distance + BANK].rearrange(natural, r=RESIDUES)
                 nc.vector.scalar_tensor_tensor(
                     out=target,
-                    in0=turned_of_unit[(h, a)][:].rearrange(permuted),
+                    in0=turned_of_unit[k][:].rearrange(permuted),
                     scalar=weights[:, h, column : column + 1],
                     in1=target,
                     op0=ALU.mult,
                     op1=ALU.add,
                 )
 
-            def finish(h, a):
-                result, sixth = tiles_of_head[h]
-                if h == last_head:
-                    short_distance(h, a, 3)
-                elif a == 0:
-                    nc.gpsimd.tensor_tensor(
-                        out=result[:, 0, 6:BANK], in0=result[:, 0, 6:BANK], in1=sixth[:, 0 : BANK - 6], op=ALU.add
-                    )
-                else:
-                    nc.gpsimd.tensor_tensor(
-                        out=result[:, 1, 0:BANK], in0=result[:, 1, 0:BANK], in1=sixth[:, BANK - 6 : TOKENS - 6], op=ALU.add
-                    )
+            def finish(k):
+                h, a = units[k]
+                result = result_of_head[h]
+                for distance, product in products_of_unit[k]:
+                    target = result[:, a, distance : distance + BANK]
+                    nc.gpsimd.tensor_tensor(out=target, in0=target, in1=product[:], op=ALU.add)
                 if a == 1:
-                    carrier = nc.vector if h == last_head else nc.gpsimd
+                    carrier = nc.vector if h == HEADS - 1 else nc.gpsimd
                     carrier.tensor_tensor(
                         out=result[:, 1, 0:PAD], in0=result[:, 1, 0:PAD], in1=result[:, 0, BANK : BANK + PAD], op=ALU.add
                     )
@@ -341,17 +346,21 @@ def tile_causalwaveletfieldattentionbyte_pa_kernel(
                         in_=result[b * HEAD_DIM : (b + 1) * HEAD_DIM, a, 0:BANK],
                     )
 
-            units = [(h, a) for h in range(HEADS) for a in range(BLOCKS)]
+            def kept(k):
+                return [which for which in range(len(short_distances)) if which not in handed_over(k)]
 
             def filter_step(k):
+                mine = []
                 if k < len(units):
-                    multiples_of_four(*units[k])
-                    short_distance(*units[k], 0)
+                    multiples_of_four(k)
+                    mine = [(k, which) for which in kept(k)[0:2]]
+                theirs = [(k - 1, which) for which in kept(k - 1)[2:]] if k > 0 else []
+                for place in range(max(len(mine), len(theirs))):
+                    for adds in (mine, theirs):
+                        if place < len(adds):
+                            short_distance(*adds[place])
                 if k > 0:
-                    short_distance(*units[k - 1], 2)
-                    finish(*units[k - 1])
-                if k < len(units):
-                    short_distance(*units[k], 1)
+                    finish(k - 1)
 
             for t in range(TOKEN_TILES):
                 project_step(1, t)

@@ -84,6 +84,55 @@ def tile_causalwaveletfieldattentionbyte_pa_kernel(
         psum_acc = ctx.enter_context(tc.psum_pool(name="psum_acc", bufs=3))
         psum_flip = ctx.enter_context(tc.psum_pool(name="psum_flip", bufs=5))
 
+        def project(acc, t, words, first_plane, channels):
+            tokens = slice(t * P, (t + 1) * P)
+            for g in range(PASSES):
+                nc.tensor.matmul_mx(
+                    out=acc,
+                    lhsT=x_codes[:, g, tokens].bitcast(FP8X4),
+                    lhsT_scale=x_planes[:, g, tokens],
+                    rhs=words[:, g, channels].bitcast(FP8X4),
+                    rhs_scale=w_planes[4 * (first_plane + g) : P, channels],
+                    start=(g == 0),
+                    stop=(g == PASSES - 1),
+                )
+
+        heads_per_bank = BANK // HEAD_DIM
+
+        def project_step(half, t):
+            if True:
+                channels = slice(half * BANK, (half + 1) * BANK)
+                heads = slice(half * heads_per_bank, (half + 1) * heads_per_bank)
+                ra, b = divmod(t, BATCH)
+                k_ps = psum_acc.tile([P, BANK], F32, tag="acc")
+                project(k_ps[:], t, k_words, 0, channels)
+                k_biased = stage.tile([P, BANK], F32)
+                nc.vector.tensor_tensor(out=k_biased[:], in0=k_ps[:], in1=k_bias[:, channels], op=ALU.add)
+                squares = stage.tile([P, BANK], F32)
+                for e in range(heads_per_bank):
+                    h = half * heads_per_bank + e
+                    nc.scalar.activation(
+                        out=squares[:, e * HEAD_DIM : (e + 1) * HEAD_DIM],
+                        in_=k_biased[:, e * HEAD_DIM : (e + 1) * HEAD_DIM],
+                        func=ACT.Square,
+                        accum_out=norm2[:, t, h : h + 1],
+                    )
+                v_ps = psum_acc.tile([P, BANK], F32, tag="acc")
+                project(v_ps[:], t, v_words, PASSES, channels)
+                nc.vector.tensor_tensor(
+                    out=field[:, ra, heads, b, :],
+                    in0=v_ps[:].rearrange("p (h c) -> p h c", c=HEAD_DIM),
+                    in1=v_bias[:, channels].rearrange("p (h c) -> p h c", c=HEAD_DIM),
+                    op=ALU.add,
+                )
+                nc.scalar.activation(out=norm[:, t, heads], in_=norm2[:, t, heads], func=ACT.Sqrt)
+                nc.gpsimd.tensor_tensor(
+                    out=field[:, ra, heads, b, :],
+                    in0=field[:, ra, heads, b, :],
+                    in1=norm[:, t, heads].unsqueeze(2).to_broadcast([P, heads_per_bank, HEAD_DIM]),
+                    op=ALU.mult,
+                )
+
         with (
             tc.tile_pool(name="early", bufs=1) as early,
             tc.tile_pool(name="stage_x", bufs=3) as stage_x,
@@ -113,6 +162,34 @@ def tile_causalwaveletfieldattentionbyte_pa_kernel(
                             )
                     load_words(0)
             load_words(1)
+
+            x_words = x_sb[:].rearrange("p ra b d -> p (ra b) d").bitcast(F32)
+            tiles_per_xt = 2
+            def x_group(group):
+                for g in range(PASSES):
+                    grouped = stage_x.tile([P, 4 * BANK], BF16, align_bytes=64)
+                    grouped_words = grouped[:].bitcast(F32).rearrange("p (n u) -> p n u", u=2)
+                    for half in range(TILES_PER_BANK // tiles_per_xt):
+                        xt = psum_flip.tile([P, 2, tiles_per_xt * P], F32, tag="flip")
+                        for u in range(2):
+                            for s in range(tiles_per_xt):
+                                t = group * TILES_PER_BANK + half * tiles_per_xt + s
+                                nc.tensor.transpose(
+                                    xt[:, u, s * P : (s + 1) * P],
+                                    x_words[:, t, 256 * g + u : 256 * (g + 1) : 2],
+                                    ident[:],
+                                )
+                        tokens = slice(half * tiles_per_xt * P, (half + 1) * tiles_per_xt * P)
+                        nc.scalar.copy(
+                            out=grouped_words[:, tokens, :], in_=xt[:].rearrange("p u n -> p n u")
+                        )
+                    cols = slice(group * BANK, (group + 1) * BANK)
+                    nc.vector.quantize_mx(
+                        out=x_codes[:, g, cols].bitcast(FP8X4), scales=x_planes[:, g, cols], in_=grouped[:]
+                    )
+
+            groups = TOKEN_TILES // TILES_PER_BANK
+            x_group(0)
 
             small_rows_f32 = early.tile([P, P], F32)
             nc.vector.tensor_copy(out=small_rows_f32[:], in_=small_rows[:])
@@ -190,82 +267,12 @@ def tile_causalwaveletfieldattentionbyte_pa_kernel(
                 shifted = flat_out[start : start + P * (pitch - 1)].rearrange("(p e) -> p e", p=P)
                 nc.sync.dma_start(out=toeplitz[:, h, :], in_=shifted[:, 0 : 2 * P])
 
-            x_words = x_sb[:].rearrange("p ra b d -> p (ra b) d").bitcast(F32)
-            tiles_per_xt = 2
-            for group in range(TOKEN_TILES // TILES_PER_BANK):
-                for g in range(PASSES):
-                    grouped = stage_x.tile([P, 4 * BANK], BF16, align_bytes=64)
-                    grouped_words = grouped[:].bitcast(F32).rearrange("p (n u) -> p n u", u=2)
-                    for half in range(TILES_PER_BANK // tiles_per_xt):
-                        xt = psum_flip.tile([P, 2, tiles_per_xt * P], F32, tag="flip")
-                        for u in range(2):
-                            for s in range(tiles_per_xt):
-                                t = group * TILES_PER_BANK + half * tiles_per_xt + s
-                                nc.tensor.transpose(
-                                    xt[:, u, s * P : (s + 1) * P],
-                                    x_words[:, t, 256 * g + u : 256 * (g + 1) : 2],
-                                    ident[:],
-                                )
-                        tokens = slice(half * tiles_per_xt * P, (half + 1) * tiles_per_xt * P)
-                        nc.scalar.copy(
-                            out=grouped_words[:, tokens, :], in_=xt[:].rearrange("p u n -> p n u")
-                        )
-                    cols = slice(group * BANK, (group + 1) * BANK)
-                    nc.vector.quantize_mx(
-                        out=x_codes[:, g, cols].bitcast(FP8X4), scales=x_planes[:, g, cols], in_=grouped[:]
-                    )
+            for group in range(groups):
+                if group + 1 < groups:
+                    x_group(group + 1)
+                for t in range(group * TILES_PER_BANK, (group + 1) * TILES_PER_BANK):
+                    project_step(0, t)
 
-        def project(acc, t, words, first_plane, channels):
-            tokens = slice(t * P, (t + 1) * P)
-            for g in range(PASSES):
-                nc.tensor.matmul_mx(
-                    out=acc,
-                    lhsT=x_codes[:, g, tokens].bitcast(FP8X4),
-                    lhsT_scale=x_planes[:, g, tokens],
-                    rhs=words[:, g, channels].bitcast(FP8X4),
-                    rhs_scale=w_planes[4 * (first_plane + g) : P, channels],
-                    start=(g == 0),
-                    stop=(g == PASSES - 1),
-                )
-
-        heads_per_bank = BANK // HEAD_DIM
-
-        def project_step(half, t):
-            if True:
-                channels = slice(half * BANK, (half + 1) * BANK)
-                heads = slice(half * heads_per_bank, (half + 1) * heads_per_bank)
-                ra, b = divmod(t, BATCH)
-                k_ps = psum_acc.tile([P, BANK], F32, tag="acc")
-                project(k_ps[:], t, k_words, 0, channels)
-                k_biased = stage.tile([P, BANK], F32)
-                nc.vector.tensor_tensor(out=k_biased[:], in0=k_ps[:], in1=k_bias[:, channels], op=ALU.add)
-                squares = stage.tile([P, BANK], F32)
-                for e in range(heads_per_bank):
-                    h = half * heads_per_bank + e
-                    nc.scalar.activation(
-                        out=squares[:, e * HEAD_DIM : (e + 1) * HEAD_DIM],
-                        in_=k_biased[:, e * HEAD_DIM : (e + 1) * HEAD_DIM],
-                        func=ACT.Square,
-                        accum_out=norm2[:, t, h : h + 1],
-                    )
-                v_ps = psum_acc.tile([P, BANK], F32, tag="acc")
-                project(v_ps[:], t, v_words, PASSES, channels)
-                nc.vector.tensor_tensor(
-                    out=field[:, ra, heads, b, :],
-                    in0=v_ps[:].rearrange("p (h c) -> p h c", c=HEAD_DIM),
-                    in1=v_bias[:, channels].rearrange("p (h c) -> p h c", c=HEAD_DIM),
-                    op=ALU.add,
-                )
-                nc.scalar.activation(out=norm[:, t, heads], in_=norm2[:, t, heads], func=ACT.Sqrt)
-                nc.gpsimd.tensor_tensor(
-                    out=field[:, ra, heads, b, :],
-                    in0=field[:, ra, heads, b, :],
-                    in1=norm[:, t, heads].unsqueeze(2).to_broadcast([P, heads_per_bank, HEAD_DIM]),
-                    op=ALU.mult,
-                )
-
-        for t in range(TOKEN_TILES):
-            project_step(0, t)
 
         with tc.tile_pool(name="late", bufs=6) as late:
             short_distances = ((1, w_pow2, 0), (2, w_pow2, 1), (3, w_three, 0), (6, w_three, 1))

@@ -267,11 +267,10 @@ def tile_causalwaveletfieldattentionbyte_pa_kernel(
                 shifted = flat_out[start : start + P * (pitch - 1)].rearrange("(p e) -> p e", p=P)
                 nc.sync.dma_start(out=toeplitz[:, h, :], in_=shifted[:, 0 : 2 * P])
 
-            for group in range(groups):
-                if group + 1 < groups:
-                    x_group(group + 1)
-                for t in range(group * TILES_PER_BANK, (group + 1) * TILES_PER_BANK):
-                    project_step(0, t)
+            for group in range(1, groups):
+                x_group(group)
+            for t in range(TOKEN_TILES):
+                project_step(0, t)
 
 
         with tc.tile_pool(name="late", bufs=6) as late:

@@ -25,6 +25,7 @@ BLOCKS = TOKENS // (RESIDUES * P)
 RA = RESIDUES * BLOCKS
 TOKEN_TILES = RA * BATCH
 TILES_PER_BANK = BANK // P
+LAG = 2
 PAD = 8
 SPREAD_ROWS = 20
 T0, T1, T2, T3 = 0.4829629131445341, 0.8365163037378079, 0.2241438680420134, -0.1294095225512604
@@ -370,6 +371,7 @@ def tile_causalwaveletfieldattentionbyte_pa_kernel(
 
             for t in range(TOKEN_TILES):
                 project_step(1, t)
-                filter_step(t)
-            for k in range(TOKEN_TILES, len(units) + 1):
+                if t >= LAG:
+                    filter_step(t - LAG)
+            for k in range(TOKEN_TILES - LAG, len(units) + 1):
                 filter_step(k)

@@ -153,15 +153,14 @@ def tile_causalwaveletfieldattentionbyte_pa_kernel(
                         out=x_sb[:, BLOCKS * r : BLOCKS * (r + 1), b, :],
                         in_=x[b].rearrange("(a i r) d -> r i a d", i=P, r=RESIDUES)[r],
                     )
-                if r == 0:
-                    for w_index, scales in enumerate((k_w_scales, v_w_scales)):
-                        for quadrant in range(4):
-                            first = 32 * quadrant + 4 * PASSES * w_index
-                            nc.sync.dma_start(
-                                out=w_planes[first : first + 4 * PASSES, :].bitcast(I32),
-                                in_=scales[:, 4 * quadrant : 4 * quadrant + 4, :].bitcast(I32),
-                            )
-                    load_words(0)
+            for w_index, scales in enumerate((k_w_scales, v_w_scales)):
+                for quadrant in range(4):
+                    first = 32 * quadrant + 4 * PASSES * w_index
+                    nc.sync.dma_start(
+                        out=w_planes[first : first + 4 * PASSES, :].bitcast(I32),
+                        in_=scales[:, 4 * quadrant : 4 * quadrant + 4, :].bitcast(I32),
+                    )
+            load_words(0)
             load_words(1)
 
             x_words = x_sb[:].rearrange("p ra b d -> p (ra b) d").bitcast(F32)

@@ -85,6 +85,9 @@ def tile_causalwaveletfieldattentionbyte_pa_kernel(
         psum_acc = ctx.enter_context(tc.psum_pool(name="psum_acc", bufs=3))
         psum_flip = ctx.enter_context(tc.psum_pool(name="psum_flip", bufs=5))
 
+        def where(t):
+            return t // (BATCH * RESIDUES), t // RESIDUES % BATCH, t % RESIDUES
+
         def project(acc, t, words, first_plane, channels):
             tokens = slice(t * P, (t + 1) * P)
             for g in range(PASSES):
@@ -104,7 +107,8 @@ def tile_causalwaveletfieldattentionbyte_pa_kernel(
             if True:
                 channels = slice(half * BANK, (half + 1) * BANK)
                 heads = slice(half * heads_per_bank, (half + 1) * heads_per_bank)
-                ra, b = divmod(t, BATCH)
+                a, b, r = where(t)
+                ra = BLOCKS * r + a
                 k_ps = psum_acc.tile([P, BANK], F32, tag="acc")
                 project(k_ps[:], t, k_words, 0, channels)
                 k_biased = stage.tile([P, BANK], F32)
@@ -136,7 +140,7 @@ def tile_causalwaveletfieldattentionbyte_pa_kernel(
 
         with (
             tc.tile_pool(name="early", bufs=1) as early,
-            tc.tile_pool(name="stage_x", bufs=3) as stage_x,
+            tc.tile_pool(name="stage_x", bufs=4) as stage_x,
         ):
             def load_words(half):
                 channels = slice(half * BANK, (half + 1) * BANK)
@@ -146,13 +150,16 @@ def tile_causalwaveletfieldattentionbyte_pa_kernel(
                         in_=packed.rearrange("g p n t -> p g (n t)").bitcast(I32)[:, :, channels],
                     )
 
-            x_sb = early.tile([P, RA, BATCH, WIDTH], BF16)
-            for r in range(RESIDUES):
-                for b in range(BATCH):
-                    nc.sync.dma_start(
-                        out=x_sb[:, BLOCKS * r : BLOCKS * (r + 1), b, :],
-                        in_=x[b].rearrange("(a i r) d -> r i a d", i=P, r=RESIDUES)[r],
-                    )
+            x_sb = early.tile([P, TOKEN_TILES, WIDTH], BF16)
+            tiles_per_load = 2
+            for first in range(0, TOKEN_TILES, tiles_per_load):
+                a, b, r = where(first)
+                nc.sync.dma_start(
+                    out=x_sb[:, first : first + tiles_per_load, :].rearrange("p t d -> p (t d)"),
+                    in_=x[b].rearrange("(a i r) d -> a i (r d)", i=P, r=RESIDUES)[a][
+                        :, r * WIDTH : (r + tiles_per_load) * WIDTH
+                    ],
+                )
             for w_index, scales in enumerate((k_w_scales, v_w_scales)):
                 for quadrant in range(4):
                     first = 32 * quadrant + 4 * PASSES * w_index
@@ -163,13 +170,15 @@ def tile_causalwaveletfieldattentionbyte_pa_kernel(
             load_words(0)
             load_words(1)
 
-            x_words = x_sb[:].rearrange("p ra b d -> p (ra b) d").bitcast(F32)
+            x_words = x_sb[:].bitcast(F32)
             tiles_per_xt = 2
             def x_group(group):
-                for g in range(PASSES):
-                    grouped = stage_x.tile([P, 4 * BANK], BF16, align_bytes=64)
-                    grouped_words = grouped[:].bitcast(F32).rearrange("p (n u) -> p n u", u=2)
-                    for half in range(TILES_PER_BANK // tiles_per_xt):
+                grouped_0 = stage_x.tile([P, 4 * BANK], BF16, align_bytes=64, tag="grouped")
+                grouped_1 = stage_x.tile([P, 4 * BANK], BF16, align_bytes=64, tag="grouped")
+                grouped_of_pass = (grouped_0, grouped_1)
+                for half in range(TILES_PER_BANK // tiles_per_xt):
+                    for g in range(PASSES):
+                        grouped_words = grouped_of_pass[g][:].bitcast(F32).rearrange("p (n u) -> p n u", u=2)
                         xt = psum_flip.tile([P, 2, tiles_per_xt * P], F32, tag="flip")
                         for u in range(2):
                             for s in range(tiles_per_xt):
@@ -183,9 +192,12 @@ def tile_causalwaveletfieldattentionbyte_pa_kernel(
                         nc.scalar.copy(
                             out=grouped_words[:, tokens, :], in_=xt[:].rearrange("p u n -> p n u")
                         )
-                    cols = slice(group * BANK, (group + 1) * BANK)
+                cols = slice(group * BANK, (group + 1) * BANK)
+                for g in range(PASSES):
                     nc.vector.quantize_mx(
-                        out=x_codes[:, g, cols].bitcast(FP8X4), scales=x_planes[:, g, cols], in_=grouped[:]
+                        out=x_codes[:, g, cols].bitcast(FP8X4),
+                        scales=x_planes[:, g, cols],
+                        in_=grouped_of_pass[g][:],
                     )
 
             groups = TOKEN_TILES // TILES_PER_BANK

@@ -25,6 +25,7 @@ BLOCKS = TOKENS // (RESIDUES * P)
 RA = RESIDUES * BLOCKS
 TOKEN_TILES = RA * BATCH
 TILES_PER_BANK = BANK // P
+AHEAD = 2
 LAG = 2
 PAD = 8
 SPREAD_ROWS = 20
@@ -103,12 +104,12 @@ def tile_causalwaveletfieldattentionbyte_pa_kernel(
 
         heads_per_bank = BANK // HEAD_DIM
 
-        def project_step(half, t):
-            if True:
-                channels = slice(half * BANK, (half + 1) * BANK)
-                heads = slice(half * heads_per_bank, (half + 1) * heads_per_bank)
-                a, b, r = where(t)
-                ra = BLOCKS * r + a
+        def project_step(half, t, parts="kv"):
+            channels = slice(half * BANK, (half + 1) * BANK)
+            heads = slice(half * heads_per_bank, (half + 1) * heads_per_bank)
+            a, b, r = where(t)
+            ra = BLOCKS * r + a
+            if "k" in parts:
                 k_ps = psum_acc.tile([P, BANK], F32, tag="acc")
                 project(k_ps[:], t, k_words, 0, channels)
                 k_biased = stage.tile([P, BANK], F32)
@@ -122,6 +123,7 @@ def tile_causalwaveletfieldattentionbyte_pa_kernel(
                         func=ACT.Square,
                         accum_out=norm2[:, t, h : h + 1],
                     )
+            if "v" in parts:
                 v_ps = psum_acc.tile([P, BANK], F32, tag="acc")
                 project(v_ps[:], t, v_words, PASSES, channels)
                 nc.vector.tensor_tensor(
@@ -209,7 +211,7 @@ def tile_causalwaveletfieldattentionbyte_pa_kernel(
             nc.tensor.transpose(small_cols_ps[:], small_rows_f32[:], ident[:])
             small_cols = early.tile([P, SPREAD_ROWS], F32)
             nc.vector.tensor_copy(out=small_cols[:], in_=small_cols_ps[:, 0:SPREAD_ROWS])
-            for bank in range(SPREAD_ROWS // TILES_PER_BANK):
+            def spread_bank(bank):
                 spread_ps = psum_flip.tile([P, TILES_PER_BANK, P], F32, tag="flip")
                 for s in range(TILES_PER_BANK):
                     row = bank * TILES_PER_BANK + s
@@ -219,6 +221,9 @@ def tile_causalwaveletfieldattentionbyte_pa_kernel(
                 nc.scalar.copy(
                     out=spread[:, bank * TILES_PER_BANK : (bank + 1) * TILES_PER_BANK, :], in_=spread_ps[:]
                 )
+
+            for bank in (4, 0, 2):
+                spread_bank(bank)
 
             logit = early.tile(gain_shape, F32)
             nc.vector.tensor_copy(out=logit[:], in_=gain_rows.rearrange("p (j h) -> p h j", h=HEADS))
@@ -281,8 +286,15 @@ def tile_causalwaveletfieldattentionbyte_pa_kernel(
 
             for group in range(1, groups):
                 x_group(group)
-            for t in range(TOKEN_TILES):
+            for t in range(AHEAD):
+                project_step(0, t, "k")
+            for t in range(AHEAD):
+                project_step(0, t, "v")
+            for t in range(AHEAD, TOKEN_TILES):
                 project_step(0, t)
+                if t == TILES_PER_BANK - 1:
+                    for bank in (1, 3):
+                        spread_bank(bank)
 
 
         with tc.tile_pool(name="late", bufs=6) as late:

from contextlib import ExitStack

import concourse.mybir as mybir
from concourse.masks import make_identity

F32 = mybir.dt.float32
BF16 = mybir.dt.bfloat16
I32 = mybir.dt.int32
U32 = mybir.dt.uint32
U8 = mybir.dt.uint8
FP8X4 = mybir.dt.float8_e4m3fn_x4
ALU = mybir.AluOpType
ACT = mybir.ActivationFunctionType
AXIS_X = mybir.AxisListType.X

P = 128
BATCH, TOKENS, WIDTH, CHANNELS, HEADS, SCALES = 2, 1024, 1024, 1024, 16, 10
HEAD_DIM = CHANNELS // HEADS
ALL_TOKENS = BATCH * TOKENS
K_PASS = 4 * P
PASSES = WIDTH // K_PASS
BANK = 512
RESIDUES = 4
BLOCKS = TOKENS // (RESIDUES * P)
RA = RESIDUES * BLOCKS
TOKEN_TILES = RA * BATCH
TILES_PER_BANK = BANK // P
AHEAD = 2
LAG = 2
PAD = 8
SPREAD_ROWS = 20
T0, T1, T2, T3 = 0.4829629131445341, 0.8365163037378079, 0.2241438680420134, -0.1294095225512604

FLOPS = 2 * ALL_TOKENS * WIDTH * 2 * CHANNELS


def tile_causalwaveletfieldattentionbyte_pa_kernel(
    tc, x, k_w_words, k_w_scales, k_b, v_w_words, v_w_scales, v_b, scale_gain, out
):
    nc = tc.nc
    with ExitStack() as ctx:
        keep = ctx.enter_context(tc.tile_pool(name="keep", bufs=1))

        w_planes = keep.tile([P, CHANNELS], U8, align_bytes=64)
        nc.vector.memset(w_planes[:].bitcast(I32), 0)

        small_rows = keep.tile([P, P], BF16)
        nc.vector.memset(small_rows[:], 0.0)
        bias_rows = CHANNELS // P
        gains_flat = scale_gain.rearrange("j h -> (j h)")
        nc.scalar.dma_start(out=small_rows[0:bias_rows, :], in_=k_b.rearrange("(row c) -> row c", c=P))
        nc.scalar.dma_start(
            out=small_rows[bias_rows : 2 * bias_rows, :], in_=v_b.rearrange("(row c) -> row c", c=P)
        )
        nc.scalar.dma_start(
            out=small_rows[2 * bias_rows : 2 * bias_rows + 1, :],
            in_=gains_flat[0:P].rearrange("(row c) -> row c", row=1),
        )
        nc.scalar.dma_start(
            out=small_rows[2 * bias_rows + 1 : 2 * bias_rows + 2, 0 : SCALES * HEADS - P],
            in_=gains_flat[P : SCALES * HEADS].rearrange("(row c) -> row c", row=1),
        )

        ident = keep.tile([P, P], F32)
        make_identity(nc, ident[:])

        x_codes = keep.tile([P, PASSES, ALL_TOKENS], U32, align_bytes=64)
        x_planes = keep.tile([P, PASSES, ALL_TOKENS], U8, align_bytes=64)
        k_words = keep.tile([P, PASSES, CHANNELS], U32, align_bytes=64)
        v_words = keep.tile([P, PASSES, CHANNELS], U32, align_bytes=64)
        toeplitz = keep.tile([P, HEADS, 2 * P], F32)
        field = keep.tile([P, RA, HEADS, BATCH, HEAD_DIM], F32)
        norm2 = keep.tile([P, TOKEN_TILES, HEADS], F32)
        norm = keep.tile([P, TOKEN_TILES, HEADS], F32)
        gain_shape = [P, HEADS, SCALES]
        spread = keep.tile([P, SPREAD_ROWS, P], F32)
        k_bias = spread[:, 0:bias_rows, :].rearrange("p row c -> p (row c)")
        v_bias = spread[:, bias_rows : 2 * bias_rows, :].rearrange("p row c -> p (row c)")
        gain_rows = spread[:, 2 * bias_rows : 2 * bias_rows + 2, :].rearrange("p row c -> p (row c)")[
            :, 0 : SCALES * HEADS
        ]
        w_pow2 = keep.tile(gain_shape, F32)
        w_three = keep.tile(gain_shape, F32)

        stage = ctx.enter_context(tc.tile_pool(name="stage", bufs=4))
        psum_acc = ctx.enter_context(tc.psum_pool(name="psum_acc", bufs=3))
        psum_flip = ctx.enter_context(tc.psum_pool(name="psum_flip", bufs=5))

        def where(t):
            return t // (BATCH * RESIDUES), t // RESIDUES % BATCH, t % RESIDUES

        def project(acc, t, words, first_plane, channels):
            tokens = slice(t * P, (t + 1) * P)
            for g in range(PASSES):
                nc.tensor.matmul_mx(
                    out=acc,
                    lhsT=x_codes[:, g, tokens].bitcast(FP8X4),
                    lhsT_scale=x_planes[:, g, tokens],
                    rhs=words[:, g, channels].bitcast(FP8X4),
                    rhs_scale=w_planes[4 * (first_plane + g) : P, channels],
                    start=(g == 0),
                    stop=(g == PASSES - 1),
                )

        heads_per_bank = BANK // HEAD_DIM

        def project_step(half, t, parts="kv"):
            channels = slice(half * BANK, (half + 1) * BANK)
            heads = slice(half * heads_per_bank, (half + 1) * heads_per_bank)
            a, b, r = where(t)
            ra = BLOCKS * r + a
            if "k" in parts:
                k_ps = psum_acc.tile([P, BANK], F32, tag="acc")
                project(k_ps[:], t, k_words, 0, channels)
                k_biased = stage.tile([P, BANK], F32)
                nc.vector.tensor_tensor(out=k_biased[:], in0=k_ps[:], in1=k_bias[:, channels], op=ALU.add)
                squares = stage.tile([P, BANK], F32)
                for e in range(heads_per_bank):
                    h = half * heads_per_bank + e
                    nc.scalar.activation(
                        out=squares[:, e * HEAD_DIM : (e + 1) * HEAD_DIM],
                        in_=k_biased[:, e * HEAD_DIM : (e + 1) * HEAD_DIM],
                        func=ACT.Square,
                        accum_out=norm2[:, t, h : h + 1],
                    )
            if "v" in parts:
                v_ps = psum_acc.tile([P, BANK], F32, tag="acc")
                project(v_ps[:], t, v_words, PASSES, channels)
                nc.vector.tensor_tensor(
                    out=field[:, ra, heads, b, :],
                    in0=v_ps[:].rearrange("p (h c) -> p h c", c=HEAD_DIM),
                    in1=v_bias[:, channels].rearrange("p (h c) -> p h c", c=HEAD_DIM),
                    op=ALU.add,
                )
                nc.scalar.activation(out=norm[:, t, heads], in_=norm2[:, t, heads], func=ACT.Sqrt)
                nc.gpsimd.tensor_tensor(
                    out=field[:, ra, heads, b, :],
                    in0=field[:, ra, heads, b, :],
                    in1=norm[:, t, heads].unsqueeze(2).to_broadcast([P, heads_per_bank, HEAD_DIM]),
                    op=ALU.mult,
                )

        with (
            tc.tile_pool(name="early", bufs=1) as early,
            tc.tile_pool(name="stage_x", bufs=4) as stage_x,
        ):
            def load_words(half):
                channels = slice(half * BANK, (half + 1) * BANK)
                for words, packed in ((k_words, k_w_words), (v_words, v_w_words)):
                    nc.sync.dma_start(
                        out=words[:, :, channels].bitcast(I32),
                        in_=packed.rearrange("g p n t -> p g (n t)").bitcast(I32)[:, :, channels],
                    )

            x_sb = early.tile([P, TOKEN_TILES, WIDTH], BF16)
            tiles_per_load = 2
            for first in range(0, TOKEN_TILES, tiles_per_load):
                a, b, r = where(first)
                nc.sync.dma_start(
                    out=x_sb[:, first : first + tiles_per_load, :].rearrange("p t d -> p (t d)"),
                    in_=x[b].rearrange("(a i r) d -> a i (r d)", i=P, r=RESIDUES)[a][
                        :, r * WIDTH : (r + tiles_per_load) * WIDTH
                    ],
                )
            for w_index, scales in enumerate((k_w_scales, v_w_scales)):
                for quadrant in range(4):
                    first = 32 * quadrant + 4 * PASSES * w_index
                    nc.sync.dma_start(
                        out=w_planes[first : first + 4 * PASSES, :].bitcast(I32),
                        in_=scales[:, 4 * quadrant : 4 * quadrant + 4, :].bitcast(I32),
                    )
            load_words(0)
            load_words(1)

            x_words = x_sb[:].bitcast(F32)
            tiles_per_xt = 2
            def x_group(group):
                grouped_0 = stage_x.tile([P, 4 * BANK], BF16, align_bytes=64, tag="grouped")
                grouped_1 = stage_x.tile([P, 4 * BANK], BF16, align_bytes=64, tag="grouped")
                grouped_of_pass = (grouped_0, grouped_1)
                for half in range(TILES_PER_BANK // tiles_per_xt):
                    for g in range(PASSES):
                        grouped_words = grouped_of_pass[g][:].bitcast(F32).rearrange("p (n u) -> p n u", u=2)
                        xt = psum_flip.tile([P, 2, tiles_per_xt * P], F32, tag="flip")
                        for u in range(2):
                            for s in range(tiles_per_xt):
                                t = group * TILES_PER_BANK + half * tiles_per_xt + s
                                nc.tensor.transpose(
                                    xt[:, u, s * P : (s + 1) * P],
                                    x_words[:, t, 256 * g + u : 256 * (g + 1) : 2],
                                    ident[:],
                                )
                        tokens = slice(half * tiles_per_xt * P, (half + 1) * tiles_per_xt * P)
                        nc.scalar.copy(
                            out=grouped_words[:, tokens, :], in_=xt[:].rearrange("p u n -> p n u")
                        )
                cols = slice(group * BANK, (group + 1) * BANK)
                for g in range(PASSES):
                    nc.vector.quantize_mx(
                        out=x_codes[:, g, cols].bitcast(FP8X4),
                        scales=x_planes[:, g, cols],
                        in_=grouped_of_pass[g][:],
                    )

            groups = TOKEN_TILES // TILES_PER_BANK
            x_group(0)

            small_rows_f32 = early.tile([P, P], F32)
            nc.vector.tensor_copy(out=small_rows_f32[:], in_=small_rows[:])
            small_cols_ps = psum_flip.tile([P, P], F32, tag="flip")
            nc.tensor.transpose(small_cols_ps[:], small_rows_f32[:], ident[:])
            small_cols = early.tile([P, SPREAD_ROWS], F32)
            nc.vector.tensor_copy(out=small_cols[:], in_=small_cols_ps[:, 0:SPREAD_ROWS])
            def spread_bank(bank):
                spread_ps = psum_flip.tile([P, TILES_PER_BANK, P], F32, tag="flip")
                for s in range(TILES_PER_BANK):
                    row = bank * TILES_PER_BANK + s
                    nc.tensor.transpose(
                        spread_ps[:, s, :], small_cols[:, row : row + 1].to_broadcast([P, P]), ident[:]
                    )
                nc.scalar.copy(
                    out=spread[:, bank * TILES_PER_BANK : (bank + 1) * TILES_PER_BANK, :], in_=spread_ps[:]
                )

            for bank in (4, 0, 2):
                spread_bank(bank)

            logit = early.tile(gain_shape, F32)
            nc.vector.tensor_copy(out=logit[:], in_=gain_rows.rearrange("p (j h) -> p h j", h=HEADS))
            top = early.tile([P, HEADS], F32)
            nc.vector.tensor_reduce(out=top[:], in_=logit[:], axis=AXIS_X, op=ALU.max)
            nc.vector.tensor_tensor(
                out=logit[:],
                in0=logit[:],
                in1=top[:].unsqueeze(2).to_broadcast(gain_shape),
                op=ALU.subtract,
            )
            expd = early.tile(gain_shape, F32)
            nc.scalar.activation(out=expd[:], in_=logit[:], func=ACT.Exp)
            total = early.tile([P, HEADS], F32)
            nc.vector.tensor_reduce(out=total[:], in_=expd[:], axis=AXIS_X, op=ALU.add)
            inverse = early.tile([P, HEADS], F32)
            nc.vector.reciprocal(out=inverse[:], in_=total[:])
            gain = early.tile(gain_shape, F32)
            nc.vector.tensor_tensor(
                out=gain[:],
                in0=expd[:],
                in1=inverse[:].unsqueeze(2).to_broadcast(gain_shape),
                op=ALU.mult,
            )
            gain_sum = early.tile([P, HEADS], F32)
            nc.vector.tensor_reduce(out=gain_sum[:], in_=gain[:], axis=AXIS_X, op=ALU.add)
            nc.vector.tensor_scalar_mul(out=w_pow2[:], in0=gain[:], scalar1=T2)
            nc.vector.scalar_tensor_tensor(
                out=w_pow2[:, :, 1:SCALES],
                in0=gain[:, :, 0 : SCALES - 1],
                scalar=T1,
                in1=w_pow2[:, :, 1:SCALES],
                op0=ALU.mult,
                op1=ALU.add,
            )
            nc.vector.tensor_scalar_mul(out=w_three[:], in0=gain[:], scalar1=T0)

            row_len = 3 * P
            weight_row = early.tile([P, HEADS, row_len], F32)
            nc.vector.memset(weight_row[:], 0.0)
            nc.gpsimd.tensor_scalar_mul(
                out=weight_row[:, :, P - 1 : P], in0=gain_sum[:].unsqueeze(2), scalar1=T3
            )
            for i in range(2, SCALES):
                at = P - 1 + 2 ** (i - 2)
                nc.gpsimd.tensor_copy(out=weight_row[:, :, at : at + 1], in_=w_pow2[:, :, i : i + 1])
            for j in range(2, SCALES - 1):
                at = P - 1 + 3 * 2 ** (j - 2)
                nc.gpsimd.tensor_copy(out=weight_row[:, :, at : at + 1], in_=w_three[:, :, j : j + 1])
            flat_out = out.rearrange("b c n -> (b c n)")
            pitch = HEADS * row_len
            nc.sync.dma_start(
                out=flat_out[0 : P * pitch].rearrange("(p e) -> p e", p=P),
                in_=weight_row[:].rearrange("p h e -> p (h e)"),
            )
            for h in range(HEADS):
                start = h * row_len + P - 1
                shifted = flat_out[start : start + P * (pitch - 1)].rearrange("(p e) -> p e", p=P)
                nc.sync.dma_start(out=toeplitz[:, h, :], in_=shifted[:, 0 : 2 * P])

            for group in range(1, groups):
                x_group(group)
            for t in range(AHEAD):
                project_step(0, t, "k")
            for t in range(AHEAD):
                project_step(0, t, "v")
            for t in range(AHEAD, TOKEN_TILES):
                project_step(0, t)
                if t == TILES_PER_BANK - 1:
                    for bank in (1, 3):
                        spread_bank(bank)


        with tc.tile_pool(name="late", bufs=6) as late:
            short_distances = ((1, w_pow2, 0), (2, w_pow2, 1), (3, w_three, 0), (6, w_three, 1))
            natural = "p (i r) -> p i r"
            permuted = "p r i -> p i r"
            units = [(h, a) for h in range(HEADS) for a in range(BLOCKS)]
            result_of_head = {}
            turned_of_unit = {}
            products_of_unit = {}

            def handed_over(k):
                if units[k][0] == HEADS - 1:
                    return ()
                return (3,)

            def multiples_of_four(k):
                h, a = units[k]
                if a == 0:
                    result = late.tile([P, BLOCKS, BANK + PAD], F32)
                    nc.gpsimd.memset(result[:, :, BANK : BANK + PAD], 0.0)
                    result_of_head[h] = result
                result = result_of_head[h]
                near = toeplitz[:, h, 0:P]
                far = toeplitz[:, h, P : 2 * P]
                block_0 = [field[:, BLOCKS * r, h].rearrange("p b c -> p (b c)") for r in range(RESIDUES)]
                block_1 = [field[:, BLOCKS * r + 1, h].rearrange("p b c -> p (b c)") for r in range(RESIDUES)]
                sums = psum_acc.tile([P, RESIDUES, P], F32, tag="acc")
                for r in range(RESIDUES):
                    if a == 0:
                        nc.tensor.matmul(out=sums[:, r, :], lhsT=block_0[r], rhs=near, start=True, stop=True)
                    else:
                        nc.tensor.matmul(out=sums[:, r, :], lhsT=block_0[r], rhs=far, start=True, stop=False)
                        nc.tensor.matmul(out=sums[:, r, :], lhsT=block_1[r], rhs=near, start=False, stop=True)
                turned = psum_flip.tile([P, RESIDUES, P], F32, tag="flip")
                for r in range(RESIDUES):
                    nc.tensor.transpose(turned[:, r, :], (block_0, block_1)[a][r], ident[:])
                turned_of_unit[k] = turned
                nc.scalar.copy(out=result[:, a, 0:BANK].rearrange(natural, r=RESIDUES), in_=sums[:].rearrange(permuted))
                products_of_unit[k] = []
                for place, which in enumerate(handed_over(k)):
                    distance, weights, column = short_distances[which]
                    product = late.tile([P, BANK], F32, tag="product%d" % place)
                    nc.scalar.activation(
                        out=product[:].rearrange(natural, r=RESIDUES),
                        in_=turned[:].rearrange(permuted),
                        func=ACT.Copy,
                        scale=weights[:, h, column : column + 1],
                    )
                    products_of_unit[k].append((distance, product))

            def short_distance(k, which):
                h, a = units[k]
                distance, weights, column = short_distances[which]
                target = result_of_head[h][:, a, distance : distance + BANK].rearrange(natural, r=RESIDUES)
                nc.vector.scalar_tensor_tensor(
                    out=target,
                    in0=turned_of_unit[k][:].rearrange(permuted),
                    scalar=weights[:, h, column : column + 1],
                    in1=target,
                    op0=ALU.mult,
                    op1=ALU.add,
                )

            def finish(k):
                h, a = units[k]
                result = result_of_head[h]
                for distance, product in products_of_unit[k]:
                    target = result[:, a, distance : distance + BANK]
                    nc.gpsimd.tensor_tensor(out=target, in0=target, in1=product[:], op=ALU.add)
                if a == 1:
                    carrier = nc.vector if h == HEADS - 1 else nc.gpsimd
                    carrier.tensor_tensor(
                        out=result[:, 1, 0:PAD], in0=result[:, 1, 0:PAD], in1=result[:, 0, BANK : BANK + PAD], op=ALU.add
                    )
                for b in range(BATCH):
                    nc.sync.dma_start(
                        out=out[b, h * HEAD_DIM : (h + 1) * HEAD_DIM, a * BANK : (a + 1) * BANK],
                        in_=result[b * HEAD_DIM : (b + 1) * HEAD_DIM, a, 0:BANK],
                    )

            def kept(k):
                return [which for which in range(len(short_distances)) if which not in handed_over(k)]

            def filter_step(k):
                mine = []
                if k < len(units):
                    multiples_of_four(k)
                    mine = [(k, which) for which in kept(k)[0:2]]
                theirs = [(k - 1, which) for which in kept(k - 1)[2:]] if k > 0 else []
                for place in range(max(len(mine), len(theirs))):
                    for adds in (mine, theirs):
                        if place < len(adds):
                            short_distance(*adds[place])
                if k > 0:
                    finish(k - 1)

            for t in range(TOKEN_TILES):
                project_step(1, t)
                if t >= LAG:
                    filter_step(t - LAG)
            for k in range(TOKEN_TILES - LAG, len(units) + 1):
                filter_step(k)
